import numpy as np
import ml_dtypes


def mxq(x, axis, fmt="e4m3"):
    dtype, down = {"e4m3": (ml_dtypes.float8_e4m3fn, 7), "e5m2": (ml_dtypes.float8_e5m2, 14)}[fmt]
    v = np.moveaxis(np.asarray(x, np.float32).astype(ml_dtypes.bfloat16).astype(np.float64), axis, -1)
    blocks = v.reshape(v.shape[:-1] + (-1, 32))
    amax = np.abs(blocks).max(-1, keepdims=True)
    byte = np.maximum(np.where(amax > 0, np.frexp(amax)[1] - 1 + 127, 0) - down, 1)
    scale = np.exp2(byte - 127.0)
    codes = (blocks / scale).astype(np.float32).astype(dtype).astype(np.float64)
    return np.moveaxis((codes * scale).reshape(v.shape), -1, axis)


WIDE = False


def mx_kscale(k):
    if not WIDE:
        return np.ones(k)
    levels = np.array([10, -10, 5, -5, 0])
    if k % 512:
        return np.exp2(np.random.permutation(np.resize(levels, k // 32))).repeat(32)
    a = np.empty((k // 512, 16))
    for p in range(k // 512):
        a[p, :8] = np.random.permutation(np.resize(levels, 8))
        for g in range(8):
            far = levels[np.abs(levels - a[p, g]) >= 10]
            a[p, g + 8] = far[np.random.randint(len(far))]
    return np.exp2(a.ravel()).repeat(32)


BF16 = ml_dtypes.bfloat16


def bf(x):
    return np.asarray(x, np.float32).astype(BF16)


def f64(x):
    return np.asarray(x).astype(np.float64)


B, DI, DH = 256, 16384, 128


def sigmoid(v):
    return 1.0 / (1.0 + np.exp(-v))


def setup_inputs():
    s = mx_kscale(DI)
    n = np.random.standard_normal
    a, c = 0.7 / np.sqrt(DI), 0.7 / np.sqrt(DH)
    keep = np.random.uniform(size=B) < 0.9
    return {
        "x": bf(n((B, DI)) * s),
        "h_minors": bf(n((B, DH))),
        "c_minors": bf(n((B, DH))),
        "s0": bf(n((B, DH))),
        "s1": bf(n((B, DH))),
        "s2": bf(n((B, DH))),
        "mask": bf(keep * (0.5 + 0.5 * np.random.uniform(size=B))),
        "weight_ih": bf(n((7 * DH, DI)) * a / s),
        "bias_ih": bf(n(7 * DH) * 0.3),
        "weight_hh": bf(n((4 * DH, DH)) * c),
        "bias_hh": bf(n(4 * DH) * 0.3),
        "weight_sh0": bf(n((DH, DH)) * c),
        "bias_sh0": bf(n(DH) * 0.3),
        "weight_sh1": bf(n((DH, DH)) * c),
        "bias_sh1": bf(n(DH) * 0.3),
        "weight_sh2": bf(n((DH, DH)) * c),
        "bias_sh2": bf(n(DH) * 0.3),
    }


def reference(x, h_minors, c_minors, s0, s1, s2, mask, weight_ih, bias_ih, weight_hh, bias_hh,
              weight_sh0, bias_sh0, weight_sh1, bias_sh1, weight_sh2, bias_sh2):
    d = DH
    m = f64(mask)[:, None]

    tmp = (mxq(f64(x), 1, "e4m3") @ mxq(f64(weight_ih), 1, "e4m3").T) + f64(bias_ih)
    tmp2 = f64(h_minors) @ f64(weight_hh).T + f64(bias_hh)
    tmp3 = np.concatenate([
        f64(s0) @ f64(weight_sh0).T + f64(bias_sh0),
        f64(s1) @ f64(weight_sh1).T + f64(bias_sh1),
        f64(s2) @ f64(weight_sh2).T + f64(bias_sh2),
    ], axis=1)

    tmp_in, tmp_s = tmp[:, :4 * d], tmp[:, 4 * d:]
    pre = tmp_in + tmp2
    ifo = sigmoid(pre[:, :3 * d])
    c_hat = pre[:, 3 * d:]
    i_g, f_g, o_g = ifo[:, :d], ifo[:, d:2 * d], ifo[:, 2 * d:]

    c_t = (f_g * f64(c_minors) + i_g * np.tanh(c_hat)) * m
    tc = np.tanh(c_t) * m
    h = o_g * tc

    bg = sigmoid(tmp_s + tmp3)
    b0, b1, b2 = bg[:, :d], bg[:, d:2 * d], bg[:, 2 * d:]

    s_0 = (b0 + 1.0 - o_g) * tc
    s_1 = (b1 + 2.0 - o_g - s_0) * 0.5 * tc
    s_2 = (b2 + 3.0 - o_g - (2.0 * s_0 + s_1)) * (1.0 / 3.0) * tc

    return (h, c_t, s_0, s_1, s_2)

@@ -1,0 +1,332 @@
+from contextlib import ExitStack
+
+import concourse.mybir as mybir
+from concourse.masks import make_identity
+
+F32 = mybir.dt.float32
+BF16 = mybir.dt.bfloat16
+I32 = mybir.dt.int32
+U32 = mybir.dt.uint32
+U8 = mybir.dt.uint8
+FP8X4 = mybir.dt.float8_e4m3fn_x4
+ALU = mybir.AluOpType
+ACT = mybir.ActivationFunctionType
+
+P = 128
+BATCH, D_IN, D_HID = 256, 16384, 128
+GATES = 7 * D_HID
+LSTM_GATES = 4 * D_HID
+
+PACK = 4
+K_PASS = P * PACK
+N_PASSES = D_IN // K_PASS
+HALVES = 2
+
+X_TILES = BATCH // P
+W_TILES = GATES // P
+ROW_TILES = X_TILES + W_TILES
+ROWS = ROW_TILES * P
+N_MOVING = 512
+COLS = X_TILES * P + 2 * N_MOVING
+
+PASSES_PER_ROUND = 2
+ROUND_K = PASSES_PER_ROUND * K_PASS
+ROUNDS = D_IN // ROUND_K
+SLAB_K = 2048
+ROUNDS_PER_SLAB = SLAB_K // ROUND_K
+SLABS = D_IN // SLAB_K
+RAW_SLABS = 2
+T_BANKS = 4
+RUNS_PER_ROUND = 3
+RUN_TILES = ROW_TILES // RUNS_PER_ROUND
+N_RUNS = ROUNDS * RUNS_PER_ROUND
+ROW_CUTS = ((0, 1024), (1024, ROWS))
+LAG = 5
+MX_BUFS = 3
+SMALL_PRODUCTS_AFTER_RUN = 7
+
+FLOPS = 2 * BATCH * GATES * D_IN + 2 * BATCH * GATES * D_HID
+
+
+def tile_share_lstm_cell_pa_k_kernel(
+    tc, x, h_minors, c_minors, s0, s1, s2, mask, weight_ih, bias_ih, weight_hh, bias_hh,
+    weight_sh0, bias_sh0, weight_sh1, bias_sh1, weight_sh2, bias_sh2,
+    out_0, out_1, out_2, out_3, out_4,
+):
+    nc = tc.nc
+    with ExitStack() as ctx:
+        ctx.enter_context(tc.manual_schedule())
+        const = ctx.enter_context(tc.tile_pool(name="const", bufs=1))
+        raw_pool = ctx.enter_context(tc.tile_pool(name="raw", bufs=RAW_SLABS * ROW_TILES))
+        grouped_pool = ctx.enter_context(tc.tile_pool(name="grouped", bufs=2))
+        tail = ctx.enter_context(tc.tile_pool(name="tail", bufs=1))
+        acc_pool = ctx.enter_context(tc.psum_pool(name="acc", bufs=1))
+        bank_pool = ctx.enter_context(tc.psum_pool(name="bank", bufs=T_BANKS))
+
+        raw_of = {}
+
+        def load(s, rt, cut, cuts):
+            if cut == 0:
+                raw_of[(s, rt)] = raw_pool.tile([P, SLAB_K], BF16, name="raw", tag="raw")
+            width = SLAB_K // cuts
+            k_cols = slice(s * SLAB_K + cut * width, s * SLAB_K + (cut + 1) * width)
+            if rt < X_TILES:
+                rows = x[rt * P : (rt + 1) * P, k_cols]
+            else:
+                rows = weight_ih[(rt - X_TILES) * P : (rt - X_TILES + 1) * P, k_cols]
+            nc.sync.dma_start(out=raw_of[(s, rt)][:, cut * width : (cut + 1) * width], in_=rows)
+
+        for cut in range(ROUNDS_PER_SLAB):
+            for rt in range(ROW_TILES):
+                load(0, rt, cut, ROUNDS_PER_SLAB)
+        for s in range(1, RAW_SLABS):
+            for rt in range(ROW_TILES):
+                load(s, rt, 0, 1)
+
+        ident_f32 = const.tile([P, P], F32)
+        make_identity(nc, ident_f32[:])
+        ident_bf16 = const.tile([P, P], BF16)
+        make_identity(nc, ident_bf16[:])
+        ones = const.tile([P, P], BF16)
+        nc.vector.memset(ones[:], 1.0)
+        warm = const.tile([P, 1], F32)
+        nc.vector.memset(warm[:], 0.0)
+        nc.scalar.activation(out=warm[:], in_=warm[:], func=ACT.Sigmoid)
+
+        mx_tiles = []
+        for n in range(MX_BUFS):
+            codes = const.tile([P, PASSES_PER_ROUND * COLS], U32, name="codes%d" % n, align_bytes=64)
+            scales = const.tile([P, PASSES_PER_ROUND * COLS], U8, name="scales%d" % n, align_bytes=64)
+            for a in range(PASSES_PER_ROUND):
+                fill = slice(a * COLS + ROWS, (a + 1) * COLS)
+                nc.vector.memset(codes[:, fill].bitcast(I32), 0)
+                nc.vector.memset(scales[:, fill].bitcast(I32), 0)
+            mx_tiles.append((codes, scales))
+
+        act_raw = const.tile([P, 4, X_TILES, D_HID], BF16)
+        for j, act in enumerate((h_minors, s0, s1, s2)):
+            nc.gpsimd.dma_start(out=act_raw[:, j, :, :], in_=act.rearrange("(t p) d -> p t d", p=P))
+        w_raw = const.tile([P, 8, D_HID], BF16)
+        nc.vector.memset(w_raw[:, 7, :], 0.0)
+        nc.gpsimd.dma_start(out=w_raw[:, 0:4, :], in_=weight_hh.rearrange("(j p) d -> p j d", p=P))
+        for j, w_sh in enumerate((weight_sh0, weight_sh1, weight_sh2)):
+            nc.gpsimd.dma_start(out=w_raw[:, 4 + j, :], in_=w_sh)
+        nc.gpsimd.dma_start(out=w_raw[0:X_TILES, 7, :], in_=mask.rearrange("(t p) -> t p", p=P))
+        bias_rows = const.tile([P, GATES], BF16)
+        nc.vector.memset(bias_rows[:], 0.0)
+        nc.gpsimd.dma_start(out=bias_rows[0:1, :], in_=bias_ih.rearrange("(o n) -> o n", o=1))
+        nc.gpsimd.dma_start(
+            out=bias_rows[1:2, 0:LSTM_GATES], in_=bias_hh.rearrange("(o n) -> o n", o=1)
+        )
+        for j, b_sh in enumerate((bias_sh0, bias_sh1, bias_sh2)):
+            cols = slice(LSTM_GATES + j * D_HID, LSTM_GATES + (j + 1) * D_HID)
+            nc.gpsimd.dma_start(out=bias_rows[1:2, cols], in_=b_sh.rearrange("(o n) -> o n", o=1))
+        c_raw = const.tile([P, X_TILES, D_HID], BF16)
+        nc.gpsimd.dma_start(out=c_raw[:], in_=c_minors.rearrange("(t p) d -> p t d", p=P))
+
+        grouped_of = {}
+
+        def transpose_run(i, run):
+            s, r = divmod(i, ROUNDS_PER_SLAB)
+            first_word = r * ROUND_K // 2
+            if run == 0:
+                grouped_of[i] = grouped_pool.tile(
+                    [P, PASSES_PER_ROUND * ROWS * PACK], BF16,
+                    name="grouped", tag="grouped", align_bytes=64,
+                )
+            grouped_words = grouped_of[i][:].bitcast(F32).rearrange(
+                "p (a r u) -> p a r u", a=PASSES_PER_ROUND, u=HALVES
+            )
+            for rt in range(run * RUN_TILES, (run + 1) * RUN_TILES):
+                words = raw_of[(s, rt)][:].bitcast(F32)
+                bank = bank_pool.tile([P, PASSES_PER_ROUND, HALVES, P], F32, tag="bank")
+                for a in range(PASSES_PER_ROUND):
+                    for u in range(HALVES):
+                        w0 = first_word + a * HALVES * P
+                        nc.tensor.transpose(
+                            bank[:, a, u, :], words[:, w0 + u : w0 + HALVES * P : HALVES], ident_f32[:]
+                        )
+                dst = grouped_words[:, :, rt * P : (rt + 1) * P, :]
+                src = bank[:].rearrange("p a u r -> p a r u")
+                if rt % RUN_TILES == 1 and run > 0:
+                    nc.vector.tensor_copy(out=dst, in_=src)
+                else:
+                    nc.scalar.copy(out=dst, in_=src)
+                if r == ROUNDS_PER_SLAB - 1 and s + RAW_SLABS < SLABS:
+                    load(s + RAW_SLABS, rt, 0, 1)
+
+        def quantise_round(i):
+            codes, scales = mx_tiles[i % MX_BUFS]
+            for lo, hi in ROW_CUTS:
+                for a in range(PASSES_PER_ROUND):
+                    nc.vector.quantize_mx(
+                        out=codes[:, a * COLS + lo : a * COLS + hi].bitcast(FP8X4),
+                        scales=scales[:, a * COLS + lo : a * COLS + hi],
+                        in_=grouped_of[i][:, (a * ROWS + lo) * PACK : (a * ROWS + hi) * PACK],
+                    )
+
+        acc = [
+            [acc_pool.tile([P, N_MOVING], F32, name="acc%d%d" % (bt, n)) for n in range(2)]
+            for bt in range(X_TILES)
+        ]
+
+        round_matmuls = [
+            (n, a, bt) for n in range(2) for a in range(PASSES_PER_ROUND) for bt in range(X_TILES)
+        ]
+        per_run = -(-len(round_matmuls) // RUNS_PER_ROUND)
+
+        def multiply_run(i, run):
+            codes, scales = mx_tiles[i % MX_BUFS]
+            for n, a, bt in round_matmuls[run * per_run : (run + 1) * per_run]:
+                c = i * PASSES_PER_ROUND + a
+                x_cols = slice(a * COLS + bt * P, a * COLS + (bt + 1) * P)
+                w0 = a * COLS + X_TILES * P + n * N_MOVING
+                w_cols = slice(w0, w0 + N_MOVING)
+                nc.tensor.matmul_mx(
+                    out=acc[bt][n][:],
+                    lhsT=codes[:, x_cols].bitcast(FP8X4),
+                    lhsT_scale=scales[:, x_cols],
+                    rhs=codes[:, w_cols].bitcast(FP8X4),
+                    rhs_scale=scales[:, w_cols],
+                    start=(c == 0),
+                    stop=(c == N_PASSES - 1),
+                )
+
+        addend = const.tile([P, X_TILES, GATES], F32)
+        mask_col = const.tile([P, X_TILES], F32)
+        c_masked = const.tile([P, X_TILES, D_HID], F32)
+
+        def small_products():
+            act_t_bank = bank_pool.tile([P, 4 * X_TILES, P], BF16, tag="bank")
+            for j in range(4):
+                for bt in range(X_TILES):
+                    nc.tensor.transpose(
+                        act_t_bank[:, j * X_TILES + bt, :], act_raw[:, j, bt, :], ident_bf16[:]
+                    )
+            act_t = const.tile([P, 4 * X_TILES, P], BF16)
+            nc.vector.tensor_copy(out=act_t[:], in_=act_t_bank[:])
+            w_t_bank = bank_pool.tile([P, 8 * D_HID], BF16, tag="bank")
+            for j in range(8):
+                nc.tensor.transpose(
+                    w_t_bank[:, j * D_HID : (j + 1) * D_HID], w_raw[:, j, :], ident_bf16[:]
+                )
+            w_t = const.tile([P, 8 * D_HID], BF16)
+            nc.scalar.copy(out=w_t[:], in_=w_t_bank[:])
+            nc.vector.tensor_copy(out=mask_col[:], in_=w_t[:, GATES : GATES + X_TILES])
+            for bt in range(X_TILES):
+                nc.vector.tensor_scalar_mul(
+                    out=c_masked[:, bt, :], in0=c_raw[:, bt, :], scalar1=mask_col[:, bt : bt + 1]
+                )
+            for bt in range(X_TILES):
+                lstm = bank_pool.tile([P, LSTM_GATES], F32, tag="bank")
+                nc.tensor.matmul(
+                    out=lstm[:], lhsT=act_t[:, bt, :], rhs=w_t[:, 0:LSTM_GATES],
+                    start=True, stop=False,
+                )
+                nc.tensor.matmul(
+                    out=lstm[:], lhsT=ones[:], rhs=bias_rows[:, 0:LSTM_GATES],
+                    start=False, stop=True,
+                )
+                nc.scalar.copy(out=addend[:, bt, 0:LSTM_GATES], in_=lstm[:])
+                shared = bank_pool.tile([P, GATES - LSTM_GATES], F32, tag="bank")
+                for j in range(3):
+                    cols = slice(LSTM_GATES + j * D_HID, LSTM_GATES + (j + 1) * D_HID)
+                    group = shared[:, j * D_HID : (j + 1) * D_HID]
+                    nc.tensor.matmul(
+                        out=group, lhsT=act_t[:, (1 + j) * X_TILES + bt, :], rhs=w_t[:, cols],
+                        start=True, stop=False,
+                    )
+                    nc.tensor.matmul(
+                        out=group, lhsT=ones[:], rhs=bias_rows[:, cols], start=False, stop=True
+                    )
+                nc.vector.tensor_copy(out=addend[:, bt, LSTM_GATES:GATES], in_=shared[:])
+
+        for turn in range(N_RUNS + LAG):
+            if turn < N_RUNS:
+                transpose_run(turn // RUNS_PER_ROUND, turn % RUNS_PER_ROUND)
+                if turn % RUNS_PER_ROUND == RUNS_PER_ROUND - 1:
+                    quantise_round(turn // RUNS_PER_ROUND)
+            if turn >= LAG:
+                multiply_run((turn - LAG) // RUNS_PER_ROUND, (turn - LAG) % RUNS_PER_ROUND)
+            if turn == SMALL_PRODUCTS_AFTER_RUN:
+                small_products()
+
+        def block(tile, j):
+            return tile[:, :, j * D_HID : (j + 1) * D_HID]
+
+        pre = tail.tile([P, X_TILES, GATES], F32)
+        gate = tail.tile([P, X_TILES, GATES], F32)
+        for bt in range(X_TILES):
+            nc.vector.tensor_add(
+                out=pre[:, bt, 0:N_MOVING], in0=acc[bt][0][:], in1=addend[:, bt, 0:N_MOVING]
+            )
+        nc.scalar.activation(out=gate[:, :, 0 : 3 * D_HID], in_=pre[:, :, 0 : 3 * D_HID], func=ACT.Sigmoid)
+        nc.scalar.activation(out=block(gate, 3), in_=block(pre, 3), func=ACT.Tanh)
+        for bt in range(X_TILES):
+            nc.vector.tensor_add(
+                out=pre[:, bt, N_MOVING:GATES],
+                in0=acc[bt][1][:, 0 : GATES - N_MOVING],
+                in1=addend[:, bt, N_MOVING:GATES],
+            )
+        nc.scalar.activation(
+            out=gate[:, :, LSTM_GATES:GATES], in_=pre[:, :, LSTM_GATES:GATES], func=ACT.Sigmoid
+        )
+        i_g, f_g, o_g, c_hat = [block(gate, j) for j in range(4)]
+
+        kept = tail.tile([P, X_TILES, D_HID], F32)
+        nc.vector.tensor_mul(out=kept[:], in0=f_g, in1=c_masked[:])
+        fresh = tail.tile([P, X_TILES, D_HID], F32)
+        for bt in range(X_TILES):
+            nc.vector.scalar_tensor_tensor(
+                out=fresh[:, bt, :], in0=i_g[:, bt, :], scalar=mask_col[:, bt : bt + 1],
+                in1=c_hat[:, bt, :], op0=ALU.mult, op1=ALU.mult,
+            )
+        c_t = tail.tile([P, X_TILES, D_HID], F32)
+        nc.vector.tensor_add(out=c_t[:], in0=kept[:], in1=fresh[:])
+        tanh_c = tail.tile([P, X_TILES, D_HID], F32)
+        nc.scalar.activation(out=tanh_c[:], in_=c_t[:], func=ACT.Tanh)
+
+        def store(out, tile):
+            nc.sync.dma_start(out=out.rearrange("(t p) d -> p t d", p=P), in_=tile[:])
+
+        store(out_1, c_t)
+        b_less_o = tail.tile([P, X_TILES, 3, D_HID], F32)
+        nc.vector.tensor_sub(
+            out=b_less_o[:],
+            in0=gate[:, :, LSTM_GATES:GATES].rearrange("p t (j d) -> p t j d", j=3),
+            in1=o_g.unsqueeze(2).to_broadcast([P, X_TILES, 3, D_HID]),
+        )
+        tc_m = tail.tile([P, X_TILES, D_HID], F32)
+        for bt in range(X_TILES):
+            nc.vector.tensor_scalar_mul(
+                out=tc_m[:, bt, :], in0=tanh_c[:, bt, :], scalar1=mask_col[:, bt : bt + 1]
+            )
+        s_0 = tail.tile([P, X_TILES, D_HID], F32)
+        nc.vector.scalar_tensor_tensor(
+            out=s_0[:], in0=b_less_o[:, :, 0, :], scalar=1.0, in1=tc_m[:], op0=ALU.add, op1=ALU.mult
+        )
+        store(out_2, s_0)
+        h = tail.tile([P, X_TILES, D_HID], F32)
+        nc.vector.tensor_mul(out=h[:], in0=o_g, in1=tc_m[:])
+        store(out_0, h)
+        rest_1 = tail.tile([P, X_TILES, D_HID], F32)
+        nc.vector.scalar_tensor_tensor(
+            out=rest_1[:], in0=b_less_o[:, :, 1, :], scalar=2.0, in1=s_0[:], op0=ALU.add, op1=ALU.subtract
+        )
+        rest_2 = tail.tile([P, X_TILES, D_HID], F32)
+        nc.vector.scalar_tensor_tensor(
+            out=rest_2[:], in0=s_0[:], scalar=-2.0, in1=b_less_o[:, :, 2, :], op0=ALU.mult, op1=ALU.add
+        )
+        s_1 = tail.tile([P, X_TILES, D_HID], F32)
+        nc.vector.scalar_tensor_tensor(
+            out=s_1[:], in0=rest_1[:], scalar=0.5, in1=tc_m[:], op0=ALU.mult, op1=ALU.mult
+        )
+        store(out_3, s_1)
+        nc.vector.scalar_tensor_tensor(
+            out=rest_2[:], in0=rest_2[:], scalar=3.0, in1=s_1[:], op0=ALU.add, op1=ALU.subtract
+        )
+        s_2 = tail.tile([P, X_TILES, D_HID], F32)
+        nc.vector.scalar_tensor_tensor(
+            out=s_2[:], in0=rest_2[:], scalar=1.0 / 3.0, in1=tc_m[:], op0=ALU.mult, op1=ALU.mult
+        )
+        store(out_4, s_2)

@@ -5,7 +5,6 @@ from concourse.masks import make_identity
 
 F32 = mybir.dt.float32
 BF16 = mybir.dt.bfloat16
-I32 = mybir.dt.int32
 U32 = mybir.dt.uint32
 U8 = mybir.dt.uint8
 FP8X4 = mybir.dt.float8_e4m3fn_x4
@@ -27,23 +26,32 @@ W_TILES = GATES // P
 ROW_TILES = X_TILES + W_TILES
 ROWS = ROW_TILES * P
 N_MOVING = 512
-COLS = X_TILES * P + 2 * N_MOVING
+COLS = ROWS
+W_STARTS = (0, GATES - N_MOVING)
 
 PASSES_PER_ROUND = 2
 ROUND_K = PASSES_PER_ROUND * K_PASS
 ROUNDS = D_IN // ROUND_K
 SLAB_K = 2048
-ROUNDS_PER_SLAB = SLAB_K // ROUND_K
-SLABS = D_IN // SLAB_K
-RAW_SLABS = 2
+FINE_K = 4 * ROUND_K
+PIECES = [(k, ROUND_K) for k in range(0, FINE_K, ROUND_K)] + [
+    (k, SLAB_K) for k in range(FINE_K, D_IN, SLAB_K)
+]
+RAW_BUFS = 10
+SORTED_BUFS = 18
+GROUP_WORDS = 8
 T_BANKS = 4
 RUNS_PER_ROUND = 3
 RUN_TILES = ROW_TILES // RUNS_PER_ROUND
 N_RUNS = ROUNDS * RUNS_PER_ROUND
 ROW_CUTS = ((0, 1024), (1024, ROWS))
-LAG = 5
-MX_BUFS = 3
-SMALL_PRODUCTS_AFTER_RUN = 7
+LAG = 6
+MX_BUFS = 2
+SORT_UNITS_PER_TURN = 4
+SORT_AHEAD = 2 * ROW_TILES + 2 * RUN_TILES
+SMALL_LOADS_AFTER = 24
+SMALL_TRANSPOSES_TURN = 15
+SMALL_PRODUCTS_TURN = 18
 
 FLOPS = 2 * BATCH * GATES * D_IN + 2 * BATCH * GATES * D_HID
 
@@ -57,31 +65,29 @@ def tile_share_lstm_cell_pa_k_kernel(
     with ExitStack() as ctx:
         ctx.enter_context(tc.manual_schedule())
         const = ctx.enter_context(tc.tile_pool(name="const", bufs=1))
-        raw_pool = ctx.enter_context(tc.tile_pool(name="raw", bufs=RAW_SLABS * ROW_TILES))
+        raw_pool = ctx.enter_context(tc.tile_pool(name="raw", bufs=RAW_BUFS))
+        sorted_pool = ctx.enter_context(tc.tile_pool(name="sorted", bufs=SORTED_BUFS))
         grouped_pool = ctx.enter_context(tc.tile_pool(name="grouped", bufs=2))
         tail = ctx.enter_context(tc.tile_pool(name="tail", bufs=1))
         acc_pool = ctx.enter_context(tc.psum_pool(name="acc", bufs=1))
         bank_pool = ctx.enter_context(tc.psum_pool(name="bank", bufs=T_BANKS))
 
+        tile_list = [(piece, rt) for piece in range(len(PIECES)) for rt in range(ROW_TILES)]
         raw_of = {}
 
-        def load(s, rt, cut, cuts):
-            if cut == 0:
-                raw_of[(s, rt)] = raw_pool.tile([P, SLAB_K], BF16, name="raw", tag="raw")
-            width = SLAB_K // cuts
-            k_cols = slice(s * SLAB_K + cut * width, s * SLAB_K + (cut + 1) * width)
+        def load(n):
+            piece, rt = tile_list[n]
+            first, width = PIECES[piece]
+            raw_of[n] = raw_pool.tile([P, width], BF16, name="raw", tag="raw")
+            k_cols = slice(first, first + width)
             if rt < X_TILES:
                 rows = x[rt * P : (rt + 1) * P, k_cols]
             else:
                 rows = weight_ih[(rt - X_TILES) * P : (rt - X_TILES + 1) * P, k_cols]
-            nc.sync.dma_start(out=raw_of[(s, rt)][:, cut * width : (cut + 1) * width], in_=rows)
+            nc.sync.dma_start(out=raw_of[n][:], in_=rows)
 
-        for cut in range(ROUNDS_PER_SLAB):
-            for rt in range(ROW_TILES):
-                load(0, rt, cut, ROUNDS_PER_SLAB)
-        for s in range(1, RAW_SLABS):
-            for rt in range(ROW_TILES):
-                load(s, rt, 0, 1)
+        for n in range(RAW_BUFS):
+            load(n)
 
         ident_f32 = const.tile([P, P], F32)
         make_identity(nc, ident_f32[:])
@@ -97,38 +103,61 @@ def tile_share_lstm_cell_pa_k_kernel(
         for n in range(MX_BUFS):
             codes = const.tile([P, PASSES_PER_ROUND * COLS], U32, name="codes%d" % n, align_bytes=64)
             scales = const.tile([P, PASSES_PER_ROUND * COLS], U8, name="scales%d" % n, align_bytes=64)
-            for a in range(PASSES_PER_ROUND):
-                fill = slice(a * COLS + ROWS, (a + 1) * COLS)
-                nc.vector.memset(codes[:, fill].bitcast(I32), 0)
-                nc.vector.memset(scales[:, fill].bitcast(I32), 0)
             mx_tiles.append((codes, scales))
 
         act_raw = const.tile([P, 4, X_TILES, D_HID], BF16)
-        for j, act in enumerate((h_minors, s0, s1, s2)):
-            nc.gpsimd.dma_start(out=act_raw[:, j, :, :], in_=act.rearrange("(t p) d -> p t d", p=P))
         w_raw = const.tile([P, 8, D_HID], BF16)
         nc.vector.memset(w_raw[:, 7, :], 0.0)
-        nc.gpsimd.dma_start(out=w_raw[:, 0:4, :], in_=weight_hh.rearrange("(j p) d -> p j d", p=P))
-        for j, w_sh in enumerate((weight_sh0, weight_sh1, weight_sh2)):
-            nc.gpsimd.dma_start(out=w_raw[:, 4 + j, :], in_=w_sh)
-        nc.gpsimd.dma_start(out=w_raw[0:X_TILES, 7, :], in_=mask.rearrange("(t p) -> t p", p=P))
         bias_rows = const.tile([P, GATES], BF16)
         nc.vector.memset(bias_rows[:], 0.0)
-        nc.gpsimd.dma_start(out=bias_rows[0:1, :], in_=bias_ih.rearrange("(o n) -> o n", o=1))
-        nc.gpsimd.dma_start(
-            out=bias_rows[1:2, 0:LSTM_GATES], in_=bias_hh.rearrange("(o n) -> o n", o=1)
-        )
-        for j, b_sh in enumerate((bias_sh0, bias_sh1, bias_sh2)):
-            cols = slice(LSTM_GATES + j * D_HID, LSTM_GATES + (j + 1) * D_HID)
-            nc.gpsimd.dma_start(out=bias_rows[1:2, cols], in_=b_sh.rearrange("(o n) -> o n", o=1))
         c_raw = const.tile([P, X_TILES, D_HID], BF16)
-        nc.gpsimd.dma_start(out=c_raw[:], in_=c_minors.rearrange("(t p) d -> p t d", p=P))
+
+        def small_loads():
+            for j, act in enumerate((h_minors, s0, s1, s2)):
+                nc.sync.dma_start(
+                    out=act_raw[:, j, :, :], in_=act.rearrange("(t p) d -> p t d", p=P)
+                )
+            nc.sync.dma_start(
+                out=w_raw[:, 0:4, :], in_=weight_hh.rearrange("(j p) d -> p j d", p=P)
+            )
+            for j, w_sh in enumerate((weight_sh0, weight_sh1, weight_sh2)):
+                nc.sync.dma_start(out=w_raw[:, 4 + j, :], in_=w_sh)
+            nc.sync.dma_start(
+                out=w_raw[0:X_TILES, 7, :], in_=mask.rearrange("(t p) -> t p", p=P)
+            )
+            nc.sync.dma_start(
+                out=bias_rows[0:1, :], in_=bias_ih.rearrange("(o n) -> o n", o=1)
+            )
+            nc.sync.dma_start(
+                out=bias_rows[1:2, 0:LSTM_GATES], in_=bias_hh.rearrange("(o n) -> o n", o=1)
+            )
+            for j, b_sh in enumerate((bias_sh0, bias_sh1, bias_sh2)):
+                cols = slice(LSTM_GATES + j * D_HID, LSTM_GATES + (j + 1) * D_HID)
+                nc.sync.dma_start(
+                    out=bias_rows[1:2, cols], in_=b_sh.rearrange("(o n) -> o n", o=1)
+                )
+            nc.sync.dma_start(out=c_raw[:], in_=c_minors.rearrange("(t p) d -> p t d", p=P))
+
+        sorted_of = {}
+
+        def sort_tile(n):
+            piece, rt = tile_list[n]
+            first, width = PIECES[piece]
+            tile = sorted_pool.tile([P, width], BF16, name="sorted", tag="sorted")
+            k_group = 2 * GROUP_WORDS
+            nc.vector.tensor_copy(
+                out=tile[:].rearrange("p (u g k) -> p u g k", u=HALVES, k=k_group),
+                in_=raw_of[n][:].rearrange("p (g u k) -> p u g k", u=HALVES, k=k_group),
+            )
+            for i in range(first // ROUND_K, (first + width) // ROUND_K):
+                sorted_of[(i, rt)] = (tile, width // 4, i - first // ROUND_K)
+            if n + RAW_BUFS < len(tile_list):
+                load(n + RAW_BUFS)
+            return width // ROUND_K
 
         grouped_of = {}
 
         def transpose_run(i, run):
-            s, r = divmod(i, ROUNDS_PER_SLAB)
-            first_word = r * ROUND_K // 2
             if run == 0:
                 grouped_of[i] = grouped_pool.tile(
                     [P, PASSES_PER_ROUND * ROWS * PACK], BF16,
@@ -138,22 +167,16 @@ def tile_share_lstm_cell_pa_k_kernel(
                 "p (a r u) -> p a r u", a=PASSES_PER_ROUND, u=HALVES
             )
             for rt in range(run * RUN_TILES, (run + 1) * RUN_TILES):
-                words = raw_of[(s, rt)][:].bitcast(F32)
+                tile, half_words, r = sorted_of[(i, rt)]
+                words = tile[:].bitcast(F32)
                 bank = bank_pool.tile([P, PASSES_PER_ROUND, HALVES, P], F32, tag="bank")
                 for a in range(PASSES_PER_ROUND):
                     for u in range(HALVES):
-                        w0 = first_word + a * HALVES * P
-                        nc.tensor.transpose(
-                            bank[:, a, u, :], words[:, w0 + u : w0 + HALVES * P : HALVES], ident_f32[:]
-                        )
+                        w0 = u * half_words + (r * PASSES_PER_ROUND + a) * P
+                        nc.tensor.transpose(bank[:, a, u, :], words[:, w0 : w0 + P], ident_f32[:])
                 dst = grouped_words[:, :, rt * P : (rt + 1) * P, :]
                 src = bank[:].rearrange("p a u r -> p a r u")
-                if rt % RUN_TILES == 1 and run > 0:
-                    nc.vector.tensor_copy(out=dst, in_=src)
-                else:
-                    nc.scalar.copy(out=dst, in_=src)
-                if r == ROUNDS_PER_SLAB - 1 and s + RAW_SLABS < SLABS:
-                    load(s + RAW_SLABS, rt, 0, 1)
+                nc.scalar.copy(out=dst, in_=src)
 
         def quantise_round(i):
             codes, scales = mx_tiles[i % MX_BUFS]
@@ -180,7 +203,7 @@ def tile_share_lstm_cell_pa_k_kernel(
             for n, a, bt in round_matmuls[run * per_run : (run + 1) * per_run]:
                 c = i * PASSES_PER_ROUND + a
                 x_cols = slice(a * COLS + bt * P, a * COLS + (bt + 1) * P)
-                w0 = a * COLS + X_TILES * P + n * N_MOVING
+                w0 = a * COLS + X_TILES * P + W_STARTS[n]
                 w_cols = slice(w0, w0 + N_MOVING)
                 nc.tensor.matmul_mx(
                     out=acc[bt][n][:],
@@ -196,60 +219,72 @@ def tile_share_lstm_cell_pa_k_kernel(
         mask_col = const.tile([P, X_TILES], F32)
         c_masked = const.tile([P, X_TILES, D_HID], F32)
 
-        def small_products():
+        act_t = const.tile([P, 4 * X_TILES, P], BF16)
+        w_t = const.tile([P, 8 * D_HID], BF16)
+
+        def small_transposes():
             act_t_bank = bank_pool.tile([P, 4 * X_TILES, P], BF16, tag="bank")
             for j in range(4):
                 for bt in range(X_TILES):
                     nc.tensor.transpose(
                         act_t_bank[:, j * X_TILES + bt, :], act_raw[:, j, bt, :], ident_bf16[:]
                     )
-            act_t = const.tile([P, 4 * X_TILES, P], BF16)
-            nc.vector.tensor_copy(out=act_t[:], in_=act_t_bank[:])
+            nc.scalar.copy(out=act_t[:], in_=act_t_bank[:])
             w_t_bank = bank_pool.tile([P, 8 * D_HID], BF16, tag="bank")
             for j in range(8):
                 nc.tensor.transpose(
                     w_t_bank[:, j * D_HID : (j + 1) * D_HID], w_raw[:, j, :], ident_bf16[:]
                 )
-            w_t = const.tile([P, 8 * D_HID], BF16)
             nc.scalar.copy(out=w_t[:], in_=w_t_bank[:])
             nc.vector.tensor_copy(out=mask_col[:], in_=w_t[:, GATES : GATES + X_TILES])
             for bt in range(X_TILES):
                 nc.vector.tensor_scalar_mul(
                     out=c_masked[:, bt, :], in0=c_raw[:, bt, :], scalar1=mask_col[:, bt : bt + 1]
                 )
-            for bt in range(X_TILES):
-                lstm = bank_pool.tile([P, LSTM_GATES], F32, tag="bank")
+
+        def small_products(bt):
+            lstm = bank_pool.tile([P, LSTM_GATES], F32, tag="bank")
+            nc.tensor.matmul(
+                out=lstm[:], lhsT=act_t[:, bt, :], rhs=w_t[:, 0:LSTM_GATES],
+                start=True, stop=False,
+            )
+            nc.tensor.matmul(
+                out=lstm[:], lhsT=ones[:], rhs=bias_rows[:, 0:LSTM_GATES],
+                start=False, stop=True,
+            )
+            nc.scalar.copy(out=addend[:, bt, 0:LSTM_GATES], in_=lstm[:])
+            shared = bank_pool.tile([P, GATES - LSTM_GATES], F32, tag="bank")
+            for j in range(3):
+                cols = slice(LSTM_GATES + j * D_HID, LSTM_GATES + (j + 1) * D_HID)
+                group = shared[:, j * D_HID : (j + 1) * D_HID]
                 nc.tensor.matmul(
-                    out=lstm[:], lhsT=act_t[:, bt, :], rhs=w_t[:, 0:LSTM_GATES],
+                    out=group, lhsT=act_t[:, (1 + j) * X_TILES + bt, :], rhs=w_t[:, cols],
                     start=True, stop=False,
                 )
                 nc.tensor.matmul(
-                    out=lstm[:], lhsT=ones[:], rhs=bias_rows[:, 0:LSTM_GATES],
-                    start=False, stop=True,
+                    out=group, lhsT=ones[:], rhs=bias_rows[:, cols], start=False, stop=True
                 )
-                nc.scalar.copy(out=addend[:, bt, 0:LSTM_GATES], in_=lstm[:])
-                shared = bank_pool.tile([P, GATES - LSTM_GATES], F32, tag="bank")
-                for j in range(3):
-                    cols = slice(LSTM_GATES + j * D_HID, LSTM_GATES + (j + 1) * D_HID)
-                    group = shared[:, j * D_HID : (j + 1) * D_HID]
-                    nc.tensor.matmul(
-                        out=group, lhsT=act_t[:, (1 + j) * X_TILES + bt, :], rhs=w_t[:, cols],
-                        start=True, stop=False,
-                    )
-                    nc.tensor.matmul(
-                        out=group, lhsT=ones[:], rhs=bias_rows[:, cols], start=False, stop=True
-                    )
-                nc.vector.tensor_copy(out=addend[:, bt, LSTM_GATES:GATES], in_=shared[:])
+            nc.scalar.copy(out=addend[:, bt, LSTM_GATES:GATES], in_=shared[:])
 
+        n_sorted = 0
+        units_sorted = 0
         for turn in range(N_RUNS + LAG):
+            units_wanted = min(RUN_TILES + turn * SORT_UNITS_PER_TURN, turn * RUN_TILES + SORT_AHEAD)
+            while n_sorted < len(tile_list) and units_sorted < units_wanted:
+                units_sorted += sort_tile(n_sorted)
+                n_sorted += 1
+                if n_sorted == SMALL_LOADS_AFTER:
+                    small_loads()
             if turn < N_RUNS:
                 transpose_run(turn // RUNS_PER_ROUND, turn % RUNS_PER_ROUND)
-                if turn % RUNS_PER_ROUND == RUNS_PER_ROUND - 1:
-                    quantise_round(turn // RUNS_PER_ROUND)
+            if turn % RUNS_PER_ROUND == 0 and 0 < turn <= N_RUNS:
+                quantise_round(turn // RUNS_PER_ROUND - 1)
             if turn >= LAG:
                 multiply_run((turn - LAG) // RUNS_PER_ROUND, (turn - LAG) % RUNS_PER_ROUND)
-            if turn == SMALL_PRODUCTS_AFTER_RUN:
-                small_products()
+            if turn == SMALL_TRANSPOSES_TURN:
+                small_transposes()
+            if 0 <= turn - SMALL_PRODUCTS_TURN < X_TILES:
+                small_products(turn - SMALL_PRODUCTS_TURN)
 
         def block(tile, j):
             return tile[:, :, j * D_HID : (j + 1) * D_HID]
@@ -265,7 +300,7 @@ def tile_share_lstm_cell_pa_k_kernel(
         for bt in range(X_TILES):
             nc.vector.tensor_add(
                 out=pre[:, bt, N_MOVING:GATES],
-                in0=acc[bt][1][:, 0 : GATES - N_MOVING],
+                in0=acc[bt][1][:, N_MOVING - (GATES - LSTM_GATES) : N_MOVING],
                 in1=addend[:, bt, N_MOVING:GATES],
             )
         nc.scalar.activation(

@@ -20,38 +20,31 @@ PACK = 4
 K_PASS = P * PACK
 N_PASSES = D_IN // K_PASS
 HALVES = 2
+GROUP_K = 16
 
 X_TILES = BATCH // P
-W_TILES = GATES // P
-ROW_TILES = X_TILES + W_TILES
-ROWS = ROW_TILES * P
-N_MOVING = 512
-COLS = ROWS
-W_STARTS = (0, GATES - N_MOVING)
-
-PASSES_PER_ROUND = 2
-ROUND_K = PASSES_PER_ROUND * K_PASS
-ROUNDS = D_IN // ROUND_K
+PAIR = 2
+PAIR_K = PAIR * K_PASS
 SLAB_K = 2048
-FINE_K = 4 * ROUND_K
-PIECES = [(k, ROUND_K) for k in range(0, FINE_K, ROUND_K)] + [
-    (k, SLAB_K) for k in range(FINE_K, D_IN, SLAB_K)
-]
+SLAB_PASSES = SLAB_K // K_PASS
+SLABS = D_IN // SLAB_K
+UNIT_WORDS = 1024
+
+X_ROWS = (0, 1)
+SWEEPS = ((2, 3, 4, 5), (6, 7), (8,))
+
 RAW_BUFS = 10
-SORTED_BUFS = 18
-GROUP_WORDS = 8
-T_BANKS = 4
-RUNS_PER_ROUND = 3
-RUN_TILES = ROW_TILES // RUNS_PER_ROUND
-N_RUNS = ROUNDS * RUNS_PER_ROUND
-ROW_CUTS = ((0, 1024), (1024, ROWS))
-LAG = 6
-MX_BUFS = 2
-SORT_UNITS_PER_TURN = 4
-SORT_AHEAD = 2 * ROW_TILES + 2 * RUN_TILES
-SMALL_LOADS_AFTER = 24
-SMALL_TRANSPOSES_TURN = 15
-SMALL_PRODUCTS_TURN = 18
+SORTED_BUFS = 12
+GROUPED_BUFS = 4
+CODE_BUFS = 4
+BANKS = 8
+LAG = 3
+SORTS_PER_TURN = 4
+SORT_GAIN_TURNS = 3
+SORT_LEAD = 4
+SMALL_LOADS_AFTER = 18
+SMALL_TRANSPOSES_TURN = 12
+SMALL_PRODUCTS_TURN = 14
 
 FLOPS = 2 * BATCH * GATES * D_IN + 2 * BATCH * GATES * D_HID
 
@@ -62,28 +55,52 @@ def tile_share_lstm_cell_pa_k_kernel(
     out_0, out_1, out_2, out_3, out_4,
 ):
     nc = tc.nc
+
+    units = []
+    for s in range(SLABS):
+        c = s * SLAB_PASSES
+        if s == 0:
+            for c in range(0, SLAB_PASSES, PAIR):
+                units += [(X_ROWS, c, PAIR), (SWEEPS[0], c, PAIR)]
+        else:
+            units += [(X_ROWS, c, SLAB_PASSES)]
+            units += [(SWEEPS[0], c + d, PAIR) for d in range(0, SLAB_PASSES, PAIR)]
+    for tiles in SWEEPS[1:]:
+        passes = UNIT_WORDS // (P * len(tiles))
+        units += [(tiles, c, passes) for c in range(0, N_PASSES, passes)]
+    last_unit = [max(u for u, unit in enumerate(units) if unit[0] == tiles) for tiles in SWEEPS]
+
+    loads = [(rt, k, PAIR_K) for k in range(0, SLAB_K, PAIR_K) for rt in X_ROWS + SWEEPS[0]]
+    loads += [(rt, k, SLAB_K) for k in range(SLAB_K, D_IN, SLAB_K) for rt in X_ROWS + SWEEPS[0]]
+    for tiles in SWEEPS[1:]:
+        loads += [(rt, k, SLAB_K) for k in range(0, D_IN, SLAB_K) for rt in tiles]
+    position = {}
+    for n, (rt, k, width) in enumerate(loads):
+        for pair in range(k // PAIR_K, (k + width) // PAIR_K):
+            position[(rt, pair)] = n
+    loads_needed = []
+    for tiles, c, passes in units:
+        last = max(position[(rt, (c + passes) // PAIR - 1)] for rt in tiles)
+        loads_needed.append(max([last + 1] + loads_needed))
+
     with ExitStack() as ctx:
         ctx.enter_context(tc.manual_schedule())
         const = ctx.enter_context(tc.tile_pool(name="const", bufs=1))
         raw_pool = ctx.enter_context(tc.tile_pool(name="raw", bufs=RAW_BUFS))
         sorted_pool = ctx.enter_context(tc.tile_pool(name="sorted", bufs=SORTED_BUFS))
-        grouped_pool = ctx.enter_context(tc.tile_pool(name="grouped", bufs=2))
-        tail = ctx.enter_context(tc.tile_pool(name="tail", bufs=1))
-        acc_pool = ctx.enter_context(tc.psum_pool(name="acc", bufs=1))
-        bank_pool = ctx.enter_context(tc.psum_pool(name="bank", bufs=T_BANKS))
+        grouped_pool = ctx.enter_context(tc.tile_pool(name="grouped", bufs=GROUPED_BUFS))
+        code_pool = ctx.enter_context(tc.tile_pool(name="code", bufs=CODE_BUFS))
+        bank_pool = ctx.enter_context(tc.psum_pool(name="bank", bufs=BANKS))
 
-        tile_list = [(piece, rt) for piece in range(len(PIECES)) for rt in range(ROW_TILES)]
         raw_of = {}
 
         def load(n):
-            piece, rt = tile_list[n]
-            first, width = PIECES[piece]
+            rt, k, width = loads[n]
             raw_of[n] = raw_pool.tile([P, width], BF16, name="raw", tag="raw")
-            k_cols = slice(first, first + width)
             if rt < X_TILES:
-                rows = x[rt * P : (rt + 1) * P, k_cols]
+                rows = x[rt * P : (rt + 1) * P, k : k + width]
             else:
-                rows = weight_ih[(rt - X_TILES) * P : (rt - X_TILES + 1) * P, k_cols]
+                rows = weight_ih[(rt - X_TILES) * P : (rt - X_TILES + 1) * P, k : k + width]
             nc.sync.dma_start(out=raw_of[n][:], in_=rows)
 
         for n in range(RAW_BUFS):
@@ -99,11 +116,8 @@ def tile_share_lstm_cell_pa_k_kernel(
         nc.vector.memset(warm[:], 0.0)
         nc.scalar.activation(out=warm[:], in_=warm[:], func=ACT.Sigmoid)
 
-        mx_tiles = []
-        for n in range(MX_BUFS):
-            codes = const.tile([P, PASSES_PER_ROUND * COLS], U32, name="codes%d" % n, align_bytes=64)
-            scales = const.tile([P, PASSES_PER_ROUND * COLS], U8, name="scales%d" % n, align_bytes=64)
-            mx_tiles.append((codes, scales))
+        x_codes = const.tile([P, N_PASSES * BATCH], U32, align_bytes=64)
+        x_scales = const.tile([P, N_PASSES * BATCH], U8, align_bytes=64)
 
         act_raw = const.tile([P, 4, X_TILES, D_HID], BF16)
         w_raw = const.tile([P, 8, D_HID], BF16)
@@ -141,119 +155,121 @@ def tile_share_lstm_cell_pa_k_kernel(
         sorted_of = {}
 
         def sort_tile(n):
-            piece, rt = tile_list[n]
-            first, width = PIECES[piece]
+            rt, k, width = loads[n]
             tile = sorted_pool.tile([P, width], BF16, name="sorted", tag="sorted")
-            k_group = 2 * GROUP_WORDS
             nc.vector.tensor_copy(
-                out=tile[:].rearrange("p (u g k) -> p u g k", u=HALVES, k=k_group),
-                in_=raw_of[n][:].rearrange("p (g u k) -> p u g k", u=HALVES, k=k_group),
+                out=tile[:].rearrange("p (h g k) -> p h g k", h=HALVES, k=GROUP_K),
+                in_=raw_of[n][:].rearrange("p (g h k) -> p h g k", h=HALVES, k=GROUP_K),
             )
-            for i in range(first // ROUND_K, (first + width) // ROUND_K):
-                sorted_of[(i, rt)] = (tile, width // 4, i - first // ROUND_K)
-            if n + RAW_BUFS < len(tile_list):
+            pairs = width // PAIR_K
+            for i in range(pairs):
+                sorted_of[(rt, k // PAIR_K + i)] = (tile, pairs, i)
+            if n + RAW_BUFS < len(loads):
                 load(n + RAW_BUFS)
-            return width // ROUND_K
 
         grouped_of = {}
 
-        def transpose_run(i, run):
-            if run == 0:
-                grouped_of[i] = grouped_pool.tile(
-                    [P, PASSES_PER_ROUND * ROWS * PACK], BF16,
-                    name="grouped", tag="grouped", align_bytes=64,
-                )
-            grouped_words = grouped_of[i][:].bitcast(F32).rearrange(
-                "p (a r u) -> p a r u", a=PASSES_PER_ROUND, u=HALVES
+        def transpose_unit(u):
+            tiles, c, passes = units[u]
+            rows = P * len(tiles)
+            grouped_of[u] = grouped_pool.tile(
+                [P, passes * rows * PACK], BF16, name="grouped", tag="grouped", align_bytes=64
             )
-            for rt in range(run * RUN_TILES, (run + 1) * RUN_TILES):
-                tile, half_words, r = sorted_of[(i, rt)]
-                words = tile[:].bitcast(F32)
-                bank = bank_pool.tile([P, PASSES_PER_ROUND, HALVES, P], F32, tag="bank")
-                for a in range(PASSES_PER_ROUND):
-                    for u in range(HALVES):
-                        w0 = u * half_words + (r * PASSES_PER_ROUND + a) * P
-                        nc.tensor.transpose(bank[:, a, u, :], words[:, w0 : w0 + P], ident_f32[:])
-                dst = grouped_words[:, :, rt * P : (rt + 1) * P, :]
-                src = bank[:].rearrange("p a u r -> p a r u")
-                nc.scalar.copy(out=dst, in_=src)
-
-        def quantise_round(i):
-            codes, scales = mx_tiles[i % MX_BUFS]
-            for lo, hi in ROW_CUTS:
-                for a in range(PASSES_PER_ROUND):
-                    nc.vector.quantize_mx(
-                        out=codes[:, a * COLS + lo : a * COLS + hi].bitcast(FP8X4),
-                        scales=scales[:, a * COLS + lo : a * COLS + hi],
-                        in_=grouped_of[i][:, (a * ROWS + lo) * PACK : (a * ROWS + hi) * PACK],
+            grouped_words = grouped_of[u][:].bitcast(F32).rearrange(
+                "p (a r h) -> p a r h", a=passes, h=HALVES
+            )
+            for a in range(0, passes, PAIR):
+                for j, rt in enumerate(tiles):
+                    tile, pairs, place = sorted_of[(rt, (c + a) // PAIR)]
+                    words = tile[:].bitcast(F32)
+                    bank = bank_pool.tile([P, PAIR, HALVES, P], F32, name="bank", tag="bank")
+                    for b in range(PAIR):
+                        for h in range(HALVES):
+                            w0 = ((h * pairs + place) * PAIR + b) * P
+                            nc.tensor.transpose(
+                                bank[:, b, h, :], words[:, w0 : w0 + P], ident_f32[:]
+                            )
+                    nc.scalar.copy(
+                        out=grouped_words[:, a : a + PAIR, j * P : (j + 1) * P, :],
+                        in_=bank[:].rearrange("p b h r -> p b r h"),
                     )
 
-        acc = [
-            [acc_pool.tile([P, N_MOVING], F32, name="acc%d%d" % (bt, n)) for n in range(2)]
-            for bt in range(X_TILES)
-        ]
+        codes_of = {}
 
-        round_matmuls = [
-            (n, a, bt) for n in range(2) for a in range(PASSES_PER_ROUND) for bt in range(X_TILES)
-        ]
-        per_run = -(-len(round_matmuls) // RUNS_PER_ROUND)
+        def quantise_unit(u):
+            tiles, c, passes = units[u]
+            n_words = passes * P * len(tiles)
+            if tiles == X_ROWS:
+                codes = x_codes[:, c * BATCH : c * BATCH + n_words]
+                scales = x_scales[:, c * BATCH : c * BATCH + n_words]
+            else:
+                w_codes = code_pool.tile([P, n_words], U32, name="w_codes", tag="codes", align_bytes=64)
+                w_scales = code_pool.tile([P, n_words], U8, name="w_scales", tag="scales", align_bytes=64)
+                codes, scales = w_codes[:], w_scales[:]
+                codes_of[u] = (w_codes, w_scales)
+            nc.vector.quantize_mx(out=codes.bitcast(FP8X4), scales=scales, in_=grouped_of[u][:])
 
-        def multiply_run(i, run):
-            codes, scales = mx_tiles[i % MX_BUFS]
-            for n, a, bt in round_matmuls[run * per_run : (run + 1) * per_run]:
-                c = i * PASSES_PER_ROUND + a
-                x_cols = slice(a * COLS + bt * P, a * COLS + (bt + 1) * P)
-                w0 = a * COLS + X_TILES * P + W_STARTS[n]
-                w_cols = slice(w0, w0 + N_MOVING)
-                nc.tensor.matmul_mx(
-                    out=acc[bt][n][:],
-                    lhsT=codes[:, x_cols].bitcast(FP8X4),
-                    lhsT_scale=scales[:, x_cols],
-                    rhs=codes[:, w_cols].bitcast(FP8X4),
-                    rhs_scale=scales[:, w_cols],
-                    start=(c == 0),
-                    stop=(c == N_PASSES - 1),
-                )
+        acc = {}
+
+        def multiply_unit(u):
+            tiles, c0, passes = units[u]
+            if tiles == X_ROWS:
+                return
+            w_codes, w_scales = codes_of[u]
+            width = P * len(tiles)
+            for a in range(passes):
+                c = c0 + a
+                for bt in range(X_TILES):
+                    if c == 0:
+                        acc[(tiles, bt)] = bank_pool.tile([P, width], F32, name="acc", tag="bank")
+                    x_cols = slice(c * BATCH + bt * P, c * BATCH + (bt + 1) * P)
+                    w_cols = slice(a * width, (a + 1) * width)
+                    nc.tensor.matmul_mx(
+                        out=acc[(tiles, bt)][:],
+                        lhsT=x_codes[:, x_cols].bitcast(FP8X4),
+                        lhsT_scale=x_scales[:, x_cols],
+                        rhs=w_codes[:, w_cols].bitcast(FP8X4),
+                        rhs_scale=w_scales[:, w_cols],
+                        start=(c == 0),
+                        stop=(c == N_PASSES - 1),
+                    )
 
         addend = const.tile([P, X_TILES, GATES], F32)
         mask_col = const.tile([P, X_TILES], F32)
         c_masked = const.tile([P, X_TILES, D_HID], F32)
-
         act_t = const.tile([P, 4 * X_TILES, P], BF16)
         w_t = const.tile([P, 8 * D_HID], BF16)
 
         def small_transposes():
-            act_t_bank = bank_pool.tile([P, 4 * X_TILES, P], BF16, tag="bank")
+            act_t_bank = bank_pool.tile([P, 4 * X_TILES, P], BF16, name="act_t_bank", tag="bank")
             for j in range(4):
                 for bt in range(X_TILES):
                     nc.tensor.transpose(
                         act_t_bank[:, j * X_TILES + bt, :], act_raw[:, j, bt, :], ident_bf16[:]
                     )
             nc.scalar.copy(out=act_t[:], in_=act_t_bank[:])
-            w_t_bank = bank_pool.tile([P, 8 * D_HID], BF16, tag="bank")
+            w_t_bank = bank_pool.tile([P, 8 * D_HID], BF16, name="w_t_bank", tag="bank")
             for j in range(8):
                 nc.tensor.transpose(
                     w_t_bank[:, j * D_HID : (j + 1) * D_HID], w_raw[:, j, :], ident_bf16[:]
                 )
             nc.scalar.copy(out=w_t[:], in_=w_t_bank[:])
-            nc.vector.tensor_copy(out=mask_col[:], in_=w_t[:, GATES : GATES + X_TILES])
-            for bt in range(X_TILES):
-                nc.vector.tensor_scalar_mul(
-                    out=c_masked[:, bt, :], in0=c_raw[:, bt, :], scalar1=mask_col[:, bt : bt + 1]
-                )
 
         def small_products(bt):
-            lstm = bank_pool.tile([P, LSTM_GATES], F32, tag="bank")
+            if bt == 0:
+                nc.vector.tensor_copy(out=mask_col[:], in_=w_t[:, GATES : GATES + X_TILES])
+            nc.vector.tensor_scalar_mul(
+                out=c_masked[:, bt, :], in0=c_raw[:, bt, :], scalar1=mask_col[:, bt : bt + 1]
+            )
+            lstm = bank_pool.tile([P, LSTM_GATES], F32, name="lstm", tag="bank")
             nc.tensor.matmul(
-                out=lstm[:], lhsT=act_t[:, bt, :], rhs=w_t[:, 0:LSTM_GATES],
-                start=True, stop=False,
+                out=lstm[:], lhsT=act_t[:, bt, :], rhs=w_t[:, 0:LSTM_GATES], start=True, stop=False
             )
             nc.tensor.matmul(
-                out=lstm[:], lhsT=ones[:], rhs=bias_rows[:, 0:LSTM_GATES],
-                start=False, stop=True,
+                out=lstm[:], lhsT=ones[:], rhs=bias_rows[:, 0:LSTM_GATES], start=False, stop=True
             )
             nc.scalar.copy(out=addend[:, bt, 0:LSTM_GATES], in_=lstm[:])
-            shared = bank_pool.tile([P, GATES - LSTM_GATES], F32, tag="bank")
+            shared = bank_pool.tile([P, GATES - LSTM_GATES], F32, name="shared", tag="bank")
             for j in range(3):
                 cols = slice(LSTM_GATES + j * D_HID, LSTM_GATES + (j + 1) * D_HID)
                 group = shared[:, j * D_HID : (j + 1) * D_HID]
@@ -266,102 +282,133 @@ def tile_share_lstm_cell_pa_k_kernel(
                 )
             nc.scalar.copy(out=addend[:, bt, LSTM_GATES:GATES], in_=shared[:])
 
-        n_sorted = 0
-        units_sorted = 0
-        for turn in range(N_RUNS + LAG):
-            units_wanted = min(RUN_TILES + turn * SORT_UNITS_PER_TURN, turn * RUN_TILES + SORT_AHEAD)
-            while n_sorted < len(tile_list) and units_sorted < units_wanted:
-                units_sorted += sort_tile(n_sorted)
-                n_sorted += 1
-                if n_sorted == SMALL_LOADS_AFTER:
-                    small_loads()
-            if turn < N_RUNS:
-                transpose_run(turn // RUNS_PER_ROUND, turn % RUNS_PER_ROUND)
-            if turn % RUNS_PER_ROUND == 0 and 0 < turn <= N_RUNS:
-                quantise_round(turn // RUNS_PER_ROUND - 1)
-            if turn >= LAG:
-                multiply_run((turn - LAG) // RUNS_PER_ROUND, (turn - LAG) % RUNS_PER_ROUND)
-            if turn == SMALL_TRANSPOSES_TURN:
-                small_transposes()
-            if 0 <= turn - SMALL_PRODUCTS_TURN < X_TILES:
-                small_products(turn - SMALL_PRODUCTS_TURN)
+        def cell_tile(name, blocks=1):
+            return const.tile([P, X_TILES, blocks * D_HID], F32, name=name)
 
         def block(tile, j):
             return tile[:, :, j * D_HID : (j + 1) * D_HID]
 
-        pre = tail.tile([P, X_TILES, GATES], F32)
-        gate = tail.tile([P, X_TILES, GATES], F32)
-        for bt in range(X_TILES):
-            nc.vector.tensor_add(
-                out=pre[:, bt, 0:N_MOVING], in0=acc[bt][0][:], in1=addend[:, bt, 0:N_MOVING]
-            )
-        nc.scalar.activation(out=gate[:, :, 0 : 3 * D_HID], in_=pre[:, :, 0 : 3 * D_HID], func=ACT.Sigmoid)
-        nc.scalar.activation(out=block(gate, 3), in_=block(pre, 3), func=ACT.Tanh)
-        for bt in range(X_TILES):
-            nc.vector.tensor_add(
-                out=pre[:, bt, N_MOVING:GATES],
-                in0=acc[bt][1][:, N_MOVING - (GATES - LSTM_GATES) : N_MOVING],
-                in1=addend[:, bt, N_MOVING:GATES],
-            )
-        nc.scalar.activation(
-            out=gate[:, :, LSTM_GATES:GATES], in_=pre[:, :, LSTM_GATES:GATES], func=ACT.Sigmoid
-        )
+        def add_small(sweep, pre):
+            tiles = SWEEPS[sweep]
+            first = (tiles[0] - X_TILES) * D_HID
+            width = len(tiles) * D_HID
+            for bt in range(X_TILES):
+                nc.vector.tensor_add(
+                    out=pre[:, bt, :], in0=acc[(tiles, bt)][:],
+                    in1=addend[:, bt, first : first + width],
+                )
+
+        def store(queue, out, tile):
+            queue.dma_start(out=out.rearrange("(t p) d -> p t d", p=P), in_=tile[:])
+
+        pre_lstm = cell_tile("pre_lstm", 4)
+        gate = cell_tile("gate", 4)
         i_g, f_g, o_g, c_hat = [block(gate, j) for j in range(4)]
+        kept, fresh, c_t, tanh_c = [cell_tile(n) for n in ("kept", "fresh", "c_t", "tanh_c")]
+        tc_m = cell_tile("tc_m")
+        h = cell_tile("h")
+        less_o = cell_tile("less_o")
+        pre_b01 = cell_tile("pre_b01", 2)
+        b01 = cell_tile("b01", 2)
+        s_0, s_1, s_2 = [cell_tile(n) for n in ("s_0", "s_1", "s_2")]
+        rest_1, rest_2 = cell_tile("rest_1"), cell_tile("rest_2")
+        pre_b2, b2 = cell_tile("pre_b2"), cell_tile("b2")
 
-        kept = tail.tile([P, X_TILES, D_HID], F32)
-        nc.vector.tensor_mul(out=kept[:], in0=f_g, in1=c_masked[:])
-        fresh = tail.tile([P, X_TILES, D_HID], F32)
-        for bt in range(X_TILES):
+        def lstm_sums():
+            add_small(0, pre_lstm)
+
+        def lstm_gates():
+            nc.scalar.activation(
+                out=gate[:, :, 0 : 3 * D_HID], in_=pre_lstm[:, :, 0 : 3 * D_HID], func=ACT.Sigmoid
+            )
+            nc.scalar.activation(out=c_hat, in_=block(pre_lstm, 3), func=ACT.Tanh)
+
+        def cell_state():
+            nc.vector.tensor_mul(out=kept[:], in0=f_g, in1=c_masked[:])
+            for bt in range(X_TILES):
+                nc.vector.scalar_tensor_tensor(
+                    out=fresh[:, bt, :], in0=i_g[:, bt, :], scalar=mask_col[:, bt : bt + 1],
+                    in1=c_hat[:, bt, :], op0=ALU.mult, op1=ALU.mult,
+                )
+            nc.vector.tensor_scalar(
+                out=less_o[:], in0=o_g, scalar1=-1.0, scalar2=1.0, op0=ALU.mult, op1=ALU.add
+            )
+            nc.vector.tensor_add(out=c_t[:], in0=kept[:], in1=fresh[:])
+            store(nc.gpsimd, out_1, c_t)
+
+        def cell_tanh():
+            nc.scalar.activation(out=tanh_c[:], in_=c_t[:], func=ACT.Tanh)
+
+        def hidden():
+            for bt in range(X_TILES):
+                nc.vector.tensor_scalar_mul(
+                    out=tc_m[:, bt, :], in0=tanh_c[:, bt, :], scalar1=mask_col[:, bt : bt + 1]
+                )
+            nc.vector.tensor_mul(out=h[:], in0=o_g, in1=tc_m[:])
+            store(nc.gpsimd, out_0, h)
+
+        def b01_sums():
+            add_small(1, pre_b01)
+
+        def b01_gates():
+            nc.scalar.activation(out=b01[:], in_=pre_b01[:], func=ACT.Sigmoid)
+
+        def shared_01():
+            for j in range(2):
+                nc.vector.tensor_add(out=block(b01, j), in0=block(b01, j), in1=less_o[:])
+            nc.vector.tensor_mul(out=s_0[:], in0=block(b01, 0), in1=tc_m[:])
+            store(nc.gpsimd, out_2, s_0)
             nc.vector.scalar_tensor_tensor(
-                out=fresh[:, bt, :], in0=i_g[:, bt, :], scalar=mask_col[:, bt : bt + 1],
-                in1=c_hat[:, bt, :], op0=ALU.mult, op1=ALU.mult,
+                out=rest_1[:], in0=block(b01, 1), scalar=1.0, in1=s_0[:], op0=ALU.add, op1=ALU.subtract
             )
-        c_t = tail.tile([P, X_TILES, D_HID], F32)
-        nc.vector.tensor_add(out=c_t[:], in0=kept[:], in1=fresh[:])
-        tanh_c = tail.tile([P, X_TILES, D_HID], F32)
-        nc.scalar.activation(out=tanh_c[:], in_=c_t[:], func=ACT.Tanh)
+            nc.vector.scalar_tensor_tensor(
+                out=rest_2[:], in0=s_0[:], scalar=-2.0, in1=less_o[:], op0=ALU.mult, op1=ALU.add
+            )
+            nc.vector.scalar_tensor_tensor(
+                out=s_1[:], in0=rest_1[:], scalar=0.5, in1=tc_m[:], op0=ALU.mult, op1=ALU.mult
+            )
+            store(nc.gpsimd, out_3, s_1)
+            nc.vector.scalar_tensor_tensor(
+                out=rest_2[:], in0=rest_2[:], scalar=2.0, in1=s_1[:], op0=ALU.add, op1=ALU.subtract
+            )
 
-        def store(out, tile):
-            nc.sync.dma_start(out=out.rearrange("(t p) d -> p t d", p=P), in_=tile[:])
+        def shared_2():
+            add_small(2, pre_b2)
+            nc.scalar.activation(out=b2[:], in_=pre_b2[:], func=ACT.Sigmoid)
+            nc.vector.tensor_add(out=rest_2[:], in0=b2[:], in1=rest_2[:])
+            nc.vector.scalar_tensor_tensor(
+                out=s_2[:], in0=rest_2[:], scalar=1.0 / 3.0, in1=tc_m[:], op0=ALU.mult, op1=ALU.mult
+            )
+            store(nc.sync, out_4, s_2)
 
-        store(out_1, c_t)
-        b_less_o = tail.tile([P, X_TILES, 3, D_HID], F32)
-        nc.vector.tensor_sub(
-            out=b_less_o[:],
-            in0=gate[:, :, LSTM_GATES:GATES].rearrange("p t (j d) -> p t j d", j=3),
-            in1=o_g.unsqueeze(2).to_broadcast([P, X_TILES, 3, D_HID]),
-        )
-        tc_m = tail.tile([P, X_TILES, D_HID], F32)
+        steps = {SMALL_TRANSPOSES_TURN: [small_transposes]}
         for bt in range(X_TILES):
-            nc.vector.tensor_scalar_mul(
-                out=tc_m[:, bt, :], in0=tanh_c[:, bt, :], scalar1=mask_col[:, bt : bt + 1]
-            )
-        s_0 = tail.tile([P, X_TILES, D_HID], F32)
-        nc.vector.scalar_tensor_tensor(
-            out=s_0[:], in0=b_less_o[:, :, 0, :], scalar=1.0, in1=tc_m[:], op0=ALU.add, op1=ALU.mult
-        )
-        store(out_2, s_0)
-        h = tail.tile([P, X_TILES, D_HID], F32)
-        nc.vector.tensor_mul(out=h[:], in0=o_g, in1=tc_m[:])
-        store(out_0, h)
-        rest_1 = tail.tile([P, X_TILES, D_HID], F32)
-        nc.vector.scalar_tensor_tensor(
-            out=rest_1[:], in0=b_less_o[:, :, 1, :], scalar=2.0, in1=s_0[:], op0=ALU.add, op1=ALU.subtract
-        )
-        rest_2 = tail.tile([P, X_TILES, D_HID], F32)
-        nc.vector.scalar_tensor_tensor(
-            out=rest_2[:], in0=s_0[:], scalar=-2.0, in1=b_less_o[:, :, 2, :], op0=ALU.mult, op1=ALU.add
-        )
-        s_1 = tail.tile([P, X_TILES, D_HID], F32)
-        nc.vector.scalar_tensor_tensor(
-            out=s_1[:], in0=rest_1[:], scalar=0.5, in1=tc_m[:], op0=ALU.mult, op1=ALU.mult
-        )
-        store(out_3, s_1)
-        nc.vector.scalar_tensor_tensor(
-            out=rest_2[:], in0=rest_2[:], scalar=3.0, in1=s_1[:], op0=ALU.add, op1=ALU.subtract
-        )
-        s_2 = tail.tile([P, X_TILES, D_HID], F32)
-        nc.vector.scalar_tensor_tensor(
-            out=s_2[:], in0=rest_2[:], scalar=1.0 / 3.0, in1=tc_m[:], op0=ALU.mult, op1=ALU.mult
-        )
-        store(out_4, s_2)
+            steps[SMALL_PRODUCTS_TURN + bt] = [lambda bt=bt: small_products(bt)]
+        for sweep, chain in enumerate((
+            (lstm_sums, lstm_gates, cell_state, cell_tanh, hidden),
+            (b01_sums, b01_gates, shared_01),
+            (shared_2,),
+        )):
+            for d, step in enumerate(chain):
+                steps.setdefault(last_unit[sweep] + LAG + d, []).append(step)
+
+        n_sorted = 0
+        halves_sorted = 0
+        for turn in range(len(units) + LAG):
+            needed_now = loads_needed[min(turn, len(units) - 1)]
+            lead = min(1 + turn / SORT_GAIN_TURNS / SORTS_PER_TURN, SORT_LEAD)
+            halves_wanted = SORTS_PER_TURN * (turn + lead)
+            while n_sorted < len(loads) and (n_sorted < needed_now or halves_sorted < halves_wanted):
+                sort_tile(n_sorted)
+                halves_sorted += loads[n_sorted][2] // PAIR_K
+                n_sorted += 1
+                if n_sorted == SMALL_LOADS_AFTER:
+                    small_loads()
+            if turn < len(units):
+                transpose_unit(turn)
+            if 0 < turn <= len(units):
+                quantise_unit(turn - 1)
+            if turn >= LAG:
+                multiply_unit(turn - LAG)
+            for step in steps.get(turn, []):
+                step()

@@ -38,13 +38,12 @@ SORTED_BUFS = 12
 GROUPED_BUFS = 4
 CODE_BUFS = 4
 BANKS = 8
-LAG = 3
+LAG = 4
 SORTS_PER_TURN = 4
-SORT_GAIN_TURNS = 3
-SORT_LEAD = 4
-SMALL_LOADS_AFTER = 18
-SMALL_TRANSPOSES_TURN = 12
-SMALL_PRODUCTS_TURN = 14
+SORT_LEAD = 1
+SMALL_LOADS_FROM = 50
+SMALL_TRANSPOSES_TURN = 26
+SMALL_PRODUCTS_TURN = 28
 
 FLOPS = 2 * BATCH * GATES * D_IN + 2 * BATCH * GATES * D_HID
 
@@ -68,6 +67,8 @@ def tile_share_lstm_cell_pa_k_kernel(
     for tiles in SWEEPS[1:]:
         passes = UNIT_WORDS // (P * len(tiles))
         units += [(tiles, c, passes) for c in range(0, N_PASSES, passes)]
+    tiles, c, passes = units.pop()
+    units += [(tiles, c + d, passes // 2) for d in (0, passes // 2)]
     last_unit = [max(u for u, unit in enumerate(units) if unit[0] == tiles) for tiles in SWEEPS]
 
     loads = [(rt, k, PAIR_K) for k in range(0, SLAB_K, PAIR_K) for rt in X_ROWS + SWEEPS[0]]
@@ -102,6 +103,9 @@ def tile_share_lstm_cell_pa_k_kernel(
             else:
                 rows = weight_ih[(rt - X_TILES) * P : (rt - X_TILES + 1) * P, k : k + width]
             nc.sync.dma_start(out=raw_of[n][:], in_=rows)
+            if 0 <= n - SMALL_LOADS_FROM < len(small_loads):
+                tile, source = small_loads[n - SMALL_LOADS_FROM]
+                nc.sync.dma_start(out=tile, in_=source)
 
         for n in range(RAW_BUFS):
             load(n)
@@ -126,31 +130,27 @@ def tile_share_lstm_cell_pa_k_kernel(
         nc.vector.memset(bias_rows[:], 0.0)
         c_raw = const.tile([P, X_TILES, D_HID], BF16)
 
-        def small_loads():
-            for j, act in enumerate((h_minors, s0, s1, s2)):
-                nc.sync.dma_start(
-                    out=act_raw[:, j, :, :], in_=act.rearrange("(t p) d -> p t d", p=P)
-                )
-            nc.sync.dma_start(
-                out=w_raw[:, 0:4, :], in_=weight_hh.rearrange("(j p) d -> p j d", p=P)
+        small_loads = [
+            (act_raw[:, j, :, :], act.rearrange("(t p) d -> p t d", p=P))
+            for j, act in enumerate((h_minors, s0, s1, s2))
+        ]
+        small_loads += [(w_raw[:, 0:4, :], weight_hh.rearrange("(j p) d -> p j d", p=P))]
+        small_loads += [
+            (w_raw[:, 4 + j, :], w_sh) for j, w_sh in enumerate((weight_sh0, weight_sh1, weight_sh2))
+        ]
+        small_loads += [
+            (w_raw[0:X_TILES, 7, :], mask.rearrange("(t p) -> t p", p=P)),
+            (bias_rows[0:1, :], bias_ih.rearrange("(o n) -> o n", o=1)),
+            (bias_rows[1:2, 0:LSTM_GATES], bias_hh.rearrange("(o n) -> o n", o=1)),
+        ]
+        small_loads += [
+            (
+                bias_rows[1:2, LSTM_GATES + j * D_HID : LSTM_GATES + (j + 1) * D_HID],
+                b_sh.rearrange("(o n) -> o n", o=1),
             )
-            for j, w_sh in enumerate((weight_sh0, weight_sh1, weight_sh2)):
-                nc.sync.dma_start(out=w_raw[:, 4 + j, :], in_=w_sh)
-            nc.sync.dma_start(
-                out=w_raw[0:X_TILES, 7, :], in_=mask.rearrange("(t p) -> t p", p=P)
-            )
-            nc.sync.dma_start(
-                out=bias_rows[0:1, :], in_=bias_ih.rearrange("(o n) -> o n", o=1)
-            )
-            nc.sync.dma_start(
-                out=bias_rows[1:2, 0:LSTM_GATES], in_=bias_hh.rearrange("(o n) -> o n", o=1)
-            )
-            for j, b_sh in enumerate((bias_sh0, bias_sh1, bias_sh2)):
-                cols = slice(LSTM_GATES + j * D_HID, LSTM_GATES + (j + 1) * D_HID)
-                nc.sync.dma_start(
-                    out=bias_rows[1:2, cols], in_=b_sh.rearrange("(o n) -> o n", o=1)
-                )
-            nc.sync.dma_start(out=c_raw[:], in_=c_minors.rearrange("(t p) d -> p t d", p=P))
+            for j, b_sh in enumerate((bias_sh0, bias_sh1, bias_sh2))
+        ]
+        small_loads += [(c_raw[:], c_minors.rearrange("(t p) d -> p t d", p=P))]
 
         sorted_of = {}
 
@@ -189,10 +189,12 @@ def tile_share_lstm_cell_pa_k_kernel(
                             nc.tensor.transpose(
                                 bank[:, b, h, :], words[:, w0 : w0 + P], ident_f32[:]
                             )
-                    nc.scalar.copy(
-                        out=grouped_words[:, a : a + PAIR, j * P : (j + 1) * P, :],
-                        in_=bank[:].rearrange("p b h r -> p b r h"),
-                    )
+                    dst = grouped_words[:, a : a + PAIR, j * P : (j + 1) * P, :]
+                    src = bank[:].rearrange("p b h r -> p b r h")
+                    if u >= len(units) - 2 and a % (2 * PAIR) == 0:
+                        nc.vector.tensor_copy(out=dst, in_=src)
+                    else:
+                        nc.scalar.copy(out=dst, in_=src)
 
         codes_of = {}
 
@@ -357,7 +359,7 @@ def tile_share_lstm_cell_pa_k_kernel(
             for j in range(2):
                 nc.vector.tensor_add(out=block(b01, j), in0=block(b01, j), in1=less_o[:])
             nc.vector.tensor_mul(out=s_0[:], in0=block(b01, 0), in1=tc_m[:])
-            store(nc.gpsimd, out_2, s_0)
+            store(nc.sync, out_2, s_0)
             nc.vector.scalar_tensor_tensor(
                 out=rest_1[:], in0=block(b01, 1), scalar=1.0, in1=s_0[:], op0=ALU.add, op1=ALU.subtract
             )
@@ -367,7 +369,7 @@ def tile_share_lstm_cell_pa_k_kernel(
             nc.vector.scalar_tensor_tensor(
                 out=s_1[:], in0=rest_1[:], scalar=0.5, in1=tc_m[:], op0=ALU.mult, op1=ALU.mult
             )
-            store(nc.gpsimd, out_3, s_1)
+            store(nc.sync, out_3, s_1)
             nc.vector.scalar_tensor_tensor(
                 out=rest_2[:], in0=rest_2[:], scalar=2.0, in1=s_1[:], op0=ALU.add, op1=ALU.subtract
             )
@@ -389,21 +391,21 @@ def tile_share_lstm_cell_pa_k_kernel(
             (b01_sums, b01_gates, shared_01),
             (shared_2,),
         )):
+            first_turn = last_unit[sweep] + LAG
+            if sweep == 0:
+                first_turn = max(first_turn, SMALL_PRODUCTS_TURN + X_TILES)
             for d, step in enumerate(chain):
-                steps.setdefault(last_unit[sweep] + LAG + d, []).append(step)
+                steps.setdefault(first_turn + d, []).append(step)
 
         n_sorted = 0
         halves_sorted = 0
         for turn in range(len(units) + LAG):
             needed_now = loads_needed[min(turn, len(units) - 1)]
-            lead = min(1 + turn / SORT_GAIN_TURNS / SORTS_PER_TURN, SORT_LEAD)
-            halves_wanted = SORTS_PER_TURN * (turn + lead)
+            halves_wanted = SORTS_PER_TURN * (turn + SORT_LEAD)
             while n_sorted < len(loads) and (n_sorted < needed_now or halves_sorted < halves_wanted):
                 sort_tile(n_sorted)
                 halves_sorted += loads[n_sorted][2] // PAIR_K
                 n_sorted += 1
-                if n_sorted == SMALL_LOADS_AFTER:
-                    small_loads()
             if turn < len(units):
                 transpose_unit(turn)
             if 0 < turn <= len(units):

@@ -20,12 +20,15 @@ PACK = 4
 K_PASS = P * PACK
 N_PASSES = D_IN // K_PASS
 HALVES = 2
+
 GROUP_K = 16
+PASS_GROUPS = K_PASS // GROUP_K
 
 X_TILES = BATCH // P
 PAIR = 2
 PAIR_K = PAIR * K_PASS
 SLAB_K = 2048
+CHUNK = 2 * SLAB_K
 SLAB_PASSES = SLAB_K // K_PASS
 SLABS = D_IN // SLAB_K
 UNIT_WORDS = 1024
@@ -33,15 +36,15 @@ UNIT_WORDS = 1024
 X_ROWS = (0, 1)
 SWEEPS = ((2, 3, 4, 5), (6, 7), (8,))
 
-RAW_BUFS = 10
-SORTED_BUFS = 12
+FINE_SLABS = 1
+RAW_BUFS = 9
+ODD_BUFS = 5
 GROUPED_BUFS = 4
 CODE_BUFS = 4
 BANKS = 8
 LAG = 4
-SORTS_PER_TURN = 4
-SORT_LEAD = 1
-SMALL_LOADS_FROM = 50
+SWAP_AHEAD = 6
+SMALL_LOADS_FROM = 32
 SMALL_TRANSPOSES_TURN = 26
 SMALL_PRODUCTS_TURN = 28
 
@@ -58,8 +61,8 @@ def tile_share_lstm_cell_pa_k_kernel(
     units = []
     for s in range(SLABS):
         c = s * SLAB_PASSES
-        if s == 0:
-            for c in range(0, SLAB_PASSES, PAIR):
+        if s < FINE_SLABS:
+            for c in range(c, c + SLAB_PASSES, PAIR):
                 units += [(X_ROWS, c, PAIR), (SWEEPS[0], c, PAIR)]
         else:
             units += [(X_ROWS, c, SLAB_PASSES)]
@@ -71,24 +74,47 @@ def tile_share_lstm_cell_pa_k_kernel(
     units += [(tiles, c + d, passes // 2) for d in (0, passes // 2)]
     last_unit = [max(u for u, unit in enumerate(units) if unit[0] == tiles) for tiles in SWEEPS]
 
-    loads = [(rt, k, PAIR_K) for k in range(0, SLAB_K, PAIR_K) for rt in X_ROWS + SWEEPS[0]]
-    loads += [(rt, k, SLAB_K) for k in range(SLAB_K, D_IN, SLAB_K) for rt in X_ROWS + SWEEPS[0]]
+    pieces = []
+    chunk = 0
+    for s in range(SLABS):
+        k = s * SLAB_K
+        if s < FINE_SLABS:
+            for i, k_half in enumerate((k, k + PAIR_K)):
+                for j, rt in enumerate(X_ROWS):
+                    pieces.append((chunk, (i * X_TILES + j) * PAIR_K, (rt,), k_half, PAIR_K))
+                for j, rt in enumerate(SWEEPS[0]):
+                    pieces.append((chunk + 1 + i, j * PAIR_K, (rt,), k_half, PAIR_K))
+        else:
+            for i, tiles in enumerate((X_ROWS, SWEEPS[0][0:2], SWEEPS[0][2:4])):
+                pieces.append((chunk + i, 0, tiles, k, SLAB_K))
+        chunk += 3
     for tiles in SWEEPS[1:]:
-        loads += [(rt, k, SLAB_K) for k in range(0, D_IN, SLAB_K) for rt in tiles]
-    position = {}
-    for n, (rt, k, width) in enumerate(loads):
-        for pair in range(k // PAIR_K, (k + width) // PAIR_K):
-            position[(rt, pair)] = n
-    loads_needed = []
+        width = CHUNK // len(tiles)
+        for k in range(0, D_IN, width):
+            pieces.append((chunk, 0, tiles, k, width))
+            chunk += 1
+    n_chunks = chunk
+    piece_of, place_of = {}, {}
+    for n, (chunk, first, tiles, k, width) in enumerate(pieces):
+        for j, rt in enumerate(tiles):
+            for d in range(0, width, PAIR_K):
+                piece_of[(rt, (k + d) // PAIR_K)] = n
+                place_of[(rt, (k + d) // PAIR_K)] = (chunk, first + j * width + d)
+    pieces_needed, chunks_done = [], []
     for tiles, c, passes in units:
-        last = max(position[(rt, (c + passes) // PAIR - 1)] for rt in tiles)
-        loads_needed.append(max([last + 1] + loads_needed))
+        last = max(piece_of[(rt, (c + passes) // PAIR - 1)] for rt in tiles)
+        pieces_needed.append(max([last + 1] + pieces_needed))
+    oldest = n_chunks
+    for tiles, c, passes in reversed(units):
+        chunks_done.append(oldest)
+        oldest = min([oldest] + [place_of[(rt, c // PAIR)][0] for rt in tiles])
+    chunks_done.reverse()
 
     with ExitStack() as ctx:
         ctx.enter_context(tc.manual_schedule())
         const = ctx.enter_context(tc.tile_pool(name="const", bufs=1))
         raw_pool = ctx.enter_context(tc.tile_pool(name="raw", bufs=RAW_BUFS))
-        sorted_pool = ctx.enter_context(tc.tile_pool(name="sorted", bufs=SORTED_BUFS))
+        odd_pool = ctx.enter_context(tc.tile_pool(name="odd", bufs=ODD_BUFS))
         grouped_pool = ctx.enter_context(tc.tile_pool(name="grouped", bufs=GROUPED_BUFS))
         code_pool = ctx.enter_context(tc.tile_pool(name="code", bufs=CODE_BUFS))
         bank_pool = ctx.enter_context(tc.psum_pool(name="bank", bufs=BANKS))
@@ -96,19 +122,29 @@ def tile_share_lstm_cell_pa_k_kernel(
         raw_of = {}
 
         def load(n):
-            rt, k, width = loads[n]
-            raw_of[n] = raw_pool.tile([P, width], BF16, name="raw", tag="raw")
-            if rt < X_TILES:
-                rows = x[rt * P : (rt + 1) * P, k : k + width]
-            else:
-                rows = weight_ih[(rt - X_TILES) * P : (rt - X_TILES + 1) * P, k : k + width]
-            nc.sync.dma_start(out=raw_of[n][:], in_=rows)
-            if 0 <= n - SMALL_LOADS_FROM < len(small_loads):
-                tile, source = small_loads[n - SMALL_LOADS_FROM]
-                nc.sync.dma_start(out=tile, in_=source)
+            chunk, first, tiles, k, width = pieces[n]
+            if chunk not in raw_of:
+                raw_of[chunk] = raw_pool.tile([P, CHUNK], BF16, name="raw", tag="raw")
+            source = x if tiles[0] < X_TILES else weight_ih
+            row = (tiles[0] if tiles[0] < X_TILES else tiles[0] - X_TILES) * P
+            rows = source[row : row + len(tiles) * P, k : k + width]
+            nc.sync.dma_start(
+                out=raw_of[chunk][:, first : first + len(tiles) * width].rearrange(
+                    "p (t k) -> p t k", t=len(tiles)
+                ),
+                in_=rows.rearrange("(t p) k -> p t k", p=P),
+            )
+            if n >= SMALL_LOADS_FROM:
+                for tile, source in small_loads[2 * (n - SMALL_LOADS_FROM) :][0:2]:
+                    nc.sync.dma_start(out=tile, in_=source)
 
-        for n in range(RAW_BUFS):
-            load(n)
+        def load_more(n, chunks):
+            while n < len(pieces) and pieces[n][0] < chunks:
+                load(n)
+                n += 1
+            return n
+
+        n_loaded = load_more(0, RAW_BUFS)
 
         ident_f32 = const.tile([P, P], F32)
         make_identity(nc, ident_f32[:])
@@ -152,20 +188,28 @@ def tile_share_lstm_cell_pa_k_kernel(
         ]
         small_loads += [(c_raw[:], c_minors.rearrange("(t p) d -> p t d", p=P))]
 
-        sorted_of = {}
+        odd_of = {}
 
-        def sort_tile(n):
-            rt, k, width = loads[n]
-            tile = sorted_pool.tile([P, width], BF16, name="sorted", tag="sorted")
-            nc.vector.tensor_copy(
-                out=tile[:].rearrange("p (h g k) -> p h g k", h=HALVES, k=GROUP_K),
-                in_=raw_of[n][:].rearrange("p (g h k) -> p h g k", h=HALVES, k=GROUP_K),
+        def groups_of(n):
+            chunk, first, tiles, k, width = pieces[n]
+            return raw_of[chunk][:, first : first + len(tiles) * width].rearrange(
+                "p (c h g e k) -> p c h g e k", h=HALVES, g=PASS_GROUPS // 4, e=2, k=GROUP_K
             )
-            pairs = width // PAIR_K
-            for i in range(pairs):
-                sorted_of[(rt, k // PAIR_K + i)] = (tile, pairs, i)
-            if n + RAW_BUFS < len(loads):
-                load(n + RAW_BUFS)
+
+        def swap_groups(n):
+            chunk, first, tiles, k, width = pieces[n]
+            if chunk not in odd_of:
+                odd_of[chunk] = odd_pool.tile([P, CHUNK // 2], BF16, name="odd", tag="odd")
+            nc.vector.tensor_copy(
+                out=odd_of[chunk][:, first // 2 : (first + len(tiles) * width) // 2].rearrange(
+                    "p (c g h k) -> p c h g k", g=PASS_GROUPS // 4, h=HALVES, k=GROUP_K
+                ),
+                in_=groups_of(n)[:, :, :, :, 1, :],
+            )
+
+        def swap_back(n):
+            groups = groups_of(n)
+            nc.vector.tensor_copy(out=groups[:, :, 0, :, 1, :], in_=groups[:, :, 1, :, 0, :])
 
         grouped_of = {}
 
@@ -180,15 +224,17 @@ def tile_share_lstm_cell_pa_k_kernel(
             )
             for a in range(0, passes, PAIR):
                 for j, rt in enumerate(tiles):
-                    tile, pairs, place = sorted_of[(rt, (c + a) // PAIR)]
-                    words = tile[:].bitcast(F32)
+                    n, place = place_of[(rt, (c + a) // PAIR)]
+                    even_words = raw_of[n][:, place : place + PAIR_K].bitcast(F32)
+                    odd_words = odd_of[n][:, place // 2 : (place + PAIR_K) // 2].bitcast(F32)
                     bank = bank_pool.tile([P, PAIR, HALVES, P], F32, name="bank", tag="bank")
                     for b in range(PAIR):
-                        for h in range(HALVES):
-                            w0 = ((h * pairs + place) * PAIR + b) * P
-                            nc.tensor.transpose(
-                                bank[:, b, h, :], words[:, w0 : w0 + P], ident_f32[:]
-                            )
+                        nc.tensor.transpose(
+                            bank[:, b, 0, :], even_words[:, 2 * b * P : (2 * b + 1) * P], ident_f32[:]
+                        )
+                        nc.tensor.transpose(
+                            bank[:, b, 1, :], odd_words[:, b * P : (b + 1) * P], ident_f32[:]
+                        )
                     dst = grouped_words[:, a : a + PAIR, j * P : (j + 1) * P, :]
                     src = bank[:].rearrange("p b h r -> p b r h")
                     if u >= len(units) - 2 and a % (2 * PAIR) == 0:
@@ -219,9 +265,9 @@ def tile_share_lstm_cell_pa_k_kernel(
                 return
             w_codes, w_scales = codes_of[u]
             width = P * len(tiles)
-            for a in range(passes):
-                c = c0 + a
-                for bt in range(X_TILES):
+            for bt in range(X_TILES):
+                for a in range(passes):
+                    c = c0 + a
                     if c == 0:
                         acc[(tiles, bt)] = bank_pool.tile([P, width], F32, name="acc", tag="bank")
                     x_cols = slice(c * BATCH + bt * P, c * BATCH + (bt + 1) * P)
@@ -326,26 +372,26 @@ def tile_share_lstm_cell_pa_k_kernel(
             nc.scalar.activation(out=c_hat, in_=block(pre_lstm, 3), func=ACT.Tanh)
 
         def cell_state():
-            nc.vector.tensor_mul(out=kept[:], in0=f_g, in1=c_masked[:])
             for bt in range(X_TILES):
                 nc.vector.scalar_tensor_tensor(
                     out=fresh[:, bt, :], in0=i_g[:, bt, :], scalar=mask_col[:, bt : bt + 1],
                     in1=c_hat[:, bt, :], op0=ALU.mult, op1=ALU.mult,
                 )
-            nc.vector.tensor_scalar(
-                out=less_o[:], in0=o_g, scalar1=-1.0, scalar2=1.0, op0=ALU.mult, op1=ALU.add
-            )
-            nc.vector.tensor_add(out=c_t[:], in0=kept[:], in1=fresh[:])
+            nc.vector.tensor_mul(out=kept[:], in0=f_g, in1=c_masked[:])
+            for bt in range(X_TILES):
+                nc.vector.tensor_add(out=c_t[:, bt, :], in0=kept[:, bt, :], in1=fresh[:, bt, :])
             store(nc.gpsimd, out_1, c_t)
 
         def cell_tanh():
             nc.scalar.activation(out=tanh_c[:], in_=c_t[:], func=ACT.Tanh)
+            nc.scalar.activation(out=less_o[:], in_=o_g, func=ACT.Identity, scale=-1.0, bias=1.0)
+            for bt in range(X_TILES):
+                nc.scalar.activation(
+                    out=tc_m[:, bt, :], in_=tanh_c[:, bt, :], func=ACT.Copy,
+                    scale=mask_col[:, bt : bt + 1],
+                )
 
         def hidden():
-            for bt in range(X_TILES):
-                nc.vector.tensor_scalar_mul(
-                    out=tc_m[:, bt, :], in0=tanh_c[:, bt, :], scalar1=mask_col[:, bt : bt + 1]
-                )
             nc.vector.tensor_mul(out=h[:], in0=o_g, in1=tc_m[:])
             store(nc.gpsimd, out_0, h)
 
@@ -355,33 +401,56 @@ def tile_share_lstm_cell_pa_k_kernel(
         def b01_gates():
             nc.scalar.activation(out=b01[:], in_=pre_b01[:], func=ACT.Sigmoid)
 
+        tiles_in_turn = range(X_TILES)
+
         def shared_01():
-            for j in range(2):
-                nc.vector.tensor_add(out=block(b01, j), in0=block(b01, j), in1=less_o[:])
-            nc.vector.tensor_mul(out=s_0[:], in0=block(b01, 0), in1=tc_m[:])
+            for bt in tiles_in_turn:
+                b_j = b01[:, bt, :].rearrange("p (j d) -> p j d", j=2)
+                nc.vector.tensor_add(
+                    out=b_j, in0=b_j,
+                    in1=less_o[:, bt, :].unsqueeze(1).to_broadcast([P, 2, D_HID]),
+                )
+            for bt in tiles_in_turn:
+                nc.vector.tensor_mul(
+                    out=s_0[:, bt, :], in0=block(b01, 0)[:, bt, :], in1=tc_m[:, bt, :]
+                )
             store(nc.sync, out_2, s_0)
-            nc.vector.scalar_tensor_tensor(
-                out=rest_1[:], in0=block(b01, 1), scalar=1.0, in1=s_0[:], op0=ALU.add, op1=ALU.subtract
-            )
-            nc.vector.scalar_tensor_tensor(
-                out=rest_2[:], in0=s_0[:], scalar=-2.0, in1=less_o[:], op0=ALU.mult, op1=ALU.add
-            )
-            nc.vector.scalar_tensor_tensor(
-                out=s_1[:], in0=rest_1[:], scalar=0.5, in1=tc_m[:], op0=ALU.mult, op1=ALU.mult
-            )
+            for bt in tiles_in_turn:
+                nc.vector.scalar_tensor_tensor(
+                    out=rest_1[:, bt, :], in0=block(b01, 1)[:, bt, :], scalar=1.0,
+                    in1=s_0[:, bt, :], op0=ALU.add, op1=ALU.subtract,
+                )
+            for bt in tiles_in_turn:
+                nc.vector.scalar_tensor_tensor(
+                    out=s_1[:, bt, :], in0=rest_1[:, bt, :], scalar=0.5, in1=tc_m[:, bt, :],
+                    op0=ALU.mult, op1=ALU.mult,
+                )
             store(nc.sync, out_3, s_1)
-            nc.vector.scalar_tensor_tensor(
-                out=rest_2[:], in0=rest_2[:], scalar=2.0, in1=s_1[:], op0=ALU.add, op1=ALU.subtract
-            )
+            for bt in tiles_in_turn:
+                nc.vector.scalar_tensor_tensor(
+                    out=rest_2[:, bt, :], in0=s_0[:, bt, :], scalar=-2.0, in1=less_o[:, bt, :],
+                    op0=ALU.mult, op1=ALU.add,
+                )
+            for bt in tiles_in_turn:
+                nc.vector.scalar_tensor_tensor(
+                    out=rest_2[:, bt, :], in0=rest_2[:, bt, :], scalar=2.0, in1=s_1[:, bt, :],
+                    op0=ALU.add, op1=ALU.subtract,
+                )
 
         def shared_2():
             add_small(2, pre_b2)
-            nc.scalar.activation(out=b2[:], in_=pre_b2[:], func=ACT.Sigmoid)
-            nc.vector.tensor_add(out=rest_2[:], in0=b2[:], in1=rest_2[:])
-            nc.vector.scalar_tensor_tensor(
-                out=s_2[:], in0=rest_2[:], scalar=1.0 / 3.0, in1=tc_m[:], op0=ALU.mult, op1=ALU.mult
-            )
-            store(nc.sync, out_4, s_2)
+            for bt in tiles_in_turn:
+                nc.scalar.activation(out=b2[:, bt, :], in_=pre_b2[:, bt, :], func=ACT.Sigmoid)
+            for bt in tiles_in_turn:
+                nc.vector.tensor_add(
+                    out=rest_2[:, bt, :], in0=b2[:, bt, :], in1=rest_2[:, bt, :]
+                )
+            for bt in tiles_in_turn:
+                nc.vector.scalar_tensor_tensor(
+                    out=s_2[:, bt, :], in0=rest_2[:, bt, :], scalar=1.0 / 3.0, in1=tc_m[:, bt, :],
+                    op0=ALU.mult, op1=ALU.mult,
+                )
+                nc.sync.dma_start(out=out_4[bt * P : (bt + 1) * P, :], in_=s_2[:, bt, :])
 
         steps = {SMALL_TRANSPOSES_TURN: [small_transposes]}
         for bt in range(X_TILES):
@@ -397,19 +466,31 @@ def tile_share_lstm_cell_pa_k_kernel(
             for d, step in enumerate(chain):
                 steps.setdefault(first_turn + d, []).append(step)
 
-        n_sorted = 0
-        halves_sorted = 0
+        n_swapped = 0
+        halves_swapped = 0
+        halves_used = 0
         for turn in range(len(units) + LAG):
-            needed_now = loads_needed[min(turn, len(units) - 1)]
-            halves_wanted = SORTS_PER_TURN * (turn + SORT_LEAD)
-            while n_sorted < len(loads) and (n_sorted < needed_now or halves_sorted < halves_wanted):
-                sort_tile(n_sorted)
-                halves_sorted += loads[n_sorted][2] // PAIR_K
-                n_sorted += 1
+            half_swapped = []
             if turn < len(units):
+                tiles, c, passes = units[turn]
+                halves_used += len(tiles) * passes // PAIR
+                while n_swapped < len(pieces) and (
+                    n_swapped < pieces_needed[turn] or halves_swapped < halves_used + SWAP_AHEAD
+                ):
+                    swap_groups(n_swapped)
+                    if n_swapped < pieces_needed[turn]:
+                        swap_back(n_swapped)
+                    else:
+                        half_swapped.append(n_swapped)
+                    chunk, first, tiles, k, width = pieces[n_swapped]
+                    halves_swapped += len(tiles) * width // PAIR_K
+                    n_swapped += 1
                 transpose_unit(turn)
+                n_loaded = load_more(n_loaded, chunks_done[turn] + RAW_BUFS)
             if 0 < turn <= len(units):
                 quantise_unit(turn - 1)
+            for n in half_swapped:
+                swap_back(n)
             if turn >= LAG:
                 multiply_unit(turn - LAG)
             for step in steps.get(turn, []):

@@ -43,8 +43,8 @@ GROUPED_BUFS = 4
 CODE_BUFS = 4
 BANKS = 8
 LAG = 4
-SWAP_AHEAD = 6
-SMALL_LOADS_FROM = 32
+SWAP_AHEAD = 8
+SMALL_LOADS_FROM = 53
 SMALL_TRANSPOSES_TURN = 26
 SMALL_PRODUCTS_TURN = 28
 
@@ -86,7 +86,7 @@ def tile_share_lstm_cell_pa_k_kernel(
                     pieces.append((chunk + 1 + i, j * PAIR_K, (rt,), k_half, PAIR_K))
         else:
             for i, tiles in enumerate((X_ROWS, SWEEPS[0][0:2], SWEEPS[0][2:4])):
-                pieces.append((chunk + i, 0, tiles, k, SLAB_K))
+                pieces += [(chunk + i, j * SLAB_K, (rt,), k, SLAB_K) for j, rt in enumerate(tiles)]
         chunk += 3
     for tiles in SWEEPS[1:]:
         width = CHUNK // len(tiles)
@@ -174,19 +174,16 @@ def tile_share_lstm_cell_pa_k_kernel(
         small_loads += [
             (w_raw[:, 4 + j, :], w_sh) for j, w_sh in enumerate((weight_sh0, weight_sh1, weight_sh2))
         ]
-        small_loads += [
-            (w_raw[0:X_TILES, 7, :], mask.rearrange("(t p) -> t p", p=P)),
-            (bias_rows[0:1, :], bias_ih.rearrange("(o n) -> o n", o=1)),
-            (bias_rows[1:2, 0:LSTM_GATES], bias_hh.rearrange("(o n) -> o n", o=1)),
-        ]
-        small_loads += [
-            (
-                bias_rows[1:2, LSTM_GATES + j * D_HID : LSTM_GATES + (j + 1) * D_HID],
-                b_sh.rearrange("(o n) -> o n", o=1),
-            )
-            for j, b_sh in enumerate((bias_sh0, bias_sh1, bias_sh2))
-        ]
         small_loads += [(c_raw[:], c_minors.rearrange("(t p) d -> p t d", p=P))]
+
+        nc.gpsimd.dma_start(out=w_raw[0:X_TILES, 7, :], in_=mask.rearrange("(t p) -> t p", p=P))
+        nc.gpsimd.dma_start(out=bias_rows[0:1, :], in_=bias_ih.rearrange("(o n) -> o n", o=1))
+        nc.gpsimd.dma_start(
+            out=bias_rows[1:2, 0:LSTM_GATES], in_=bias_hh.rearrange("(o n) -> o n", o=1)
+        )
+        for j, b_sh in enumerate((bias_sh0, bias_sh1, bias_sh2)):
+            cols = slice(LSTM_GATES + j * D_HID, LSTM_GATES + (j + 1) * D_HID)
+            nc.gpsimd.dma_start(out=bias_rows[1:2, cols], in_=b_sh.rearrange("(o n) -> o n", o=1))
 
         odd_of = {}
 
@@ -478,6 +475,9 @@ def tile_share_lstm_cell_pa_k_kernel(
                     n_swapped < pieces_needed[turn] or halves_swapped < halves_used + SWAP_AHEAD
                 ):
                     swap_groups(n_swapped)
+                    for n in half_swapped:
+                        swap_back(n)
+                    half_swapped = []
                     if n_swapped < pieces_needed[turn]:
                         swap_back(n_swapped)
                     else:

@@ -40,9 +40,10 @@ FINE_SLABS = 1
 RAW_BUFS = 9
 ODD_BUFS = 5
 GROUPED_BUFS = 4
-CODE_BUFS = 4
+CODE_BUFS = 5
 BANKS = 8
 LAG = 4
+FIRST_SWEEP_JOBS = 3
 SWAP_AHEAD = 8
 SMALL_LOADS_FROM = 53
 SMALL_TRANSPOSES_TURN = 26
@@ -256,28 +257,30 @@ def tile_share_lstm_cell_pa_k_kernel(
 
         acc = {}
 
-        def multiply_unit(u):
-            tiles, c0, passes = units[u]
+        def jobs_of_unit(u):
+            tiles, c, passes = units[u]
             if tiles == X_ROWS:
-                return
+                return []
+            return [(u, bt, a) for bt in range(X_TILES) for a in range(passes)]
+
+        def multiply(u, bt, a):
+            tiles, c, passes = units[u]
+            c += a
             w_codes, w_scales = codes_of[u]
             width = P * len(tiles)
-            for bt in range(X_TILES):
-                for a in range(passes):
-                    c = c0 + a
-                    if c == 0:
-                        acc[(tiles, bt)] = bank_pool.tile([P, width], F32, name="acc", tag="bank")
-                    x_cols = slice(c * BATCH + bt * P, c * BATCH + (bt + 1) * P)
-                    w_cols = slice(a * width, (a + 1) * width)
-                    nc.tensor.matmul_mx(
-                        out=acc[(tiles, bt)][:],
-                        lhsT=x_codes[:, x_cols].bitcast(FP8X4),
-                        lhsT_scale=x_scales[:, x_cols],
-                        rhs=w_codes[:, w_cols].bitcast(FP8X4),
-                        rhs_scale=w_scales[:, w_cols],
-                        start=(c == 0),
-                        stop=(c == N_PASSES - 1),
-                    )
+            if c == 0:
+                acc[(tiles, bt)] = bank_pool.tile([P, width], F32, name="acc", tag="bank")
+            x_cols = slice(c * BATCH + bt * P, c * BATCH + (bt + 1) * P)
+            w_cols = slice(a * width, (a + 1) * width)
+            nc.tensor.matmul_mx(
+                out=acc[(tiles, bt)][:],
+                lhsT=x_codes[:, x_cols].bitcast(FP8X4),
+                lhsT_scale=x_scales[:, x_cols],
+                rhs=w_codes[:, w_cols].bitcast(FP8X4),
+                rhs_scale=w_scales[:, w_cols],
+                start=(c == 0),
+                stop=(c == N_PASSES - 1),
+            )
 
         addend = const.tile([P, X_TILES, GATES], F32)
         mask_col = const.tile([P, X_TILES], F32)
@@ -463,6 +466,7 @@ def tile_share_lstm_cell_pa_k_kernel(
             for d, step in enumerate(chain):
                 steps.setdefault(first_turn + d, []).append(step)
 
+        jobs = []
         n_swapped = 0
         halves_swapped = 0
         halves_used = 0
@@ -492,6 +496,10 @@ def tile_share_lstm_cell_pa_k_kernel(
             for n in half_swapped:
                 swap_back(n)
             if turn >= LAG:
-                multiply_unit(turn - LAG)
+                jobs += jobs_of_unit(turn - LAG)
+            n_jobs = FIRST_SWEEP_JOBS if turn - LAG < last_unit[0] else len(jobs)
+            for job in jobs[:n_jobs]:
+                multiply(*job)
+            jobs = jobs[n_jobs:]
             for step in steps.get(turn, []):
                 step()

from contextlib import ExitStack

import concourse.mybir as mybir
from concourse.masks import make_identity

F32 = mybir.dt.float32
BF16 = mybir.dt.bfloat16
U32 = mybir.dt.uint32
U8 = mybir.dt.uint8
FP8X4 = mybir.dt.float8_e4m3fn_x4
ALU = mybir.AluOpType
ACT = mybir.ActivationFunctionType

P = 128
BATCH, D_IN, D_HID = 256, 16384, 128
GATES = 7 * D_HID
LSTM_GATES = 4 * D_HID

PACK = 4
K_PASS = P * PACK
N_PASSES = D_IN // K_PASS
HALVES = 2

GROUP_K = 16
PASS_GROUPS = K_PASS // GROUP_K

X_TILES = BATCH // P
PAIR = 2
PAIR_K = PAIR * K_PASS
SLAB_K = 2048
CHUNK = 2 * SLAB_K
SLAB_PASSES = SLAB_K // K_PASS
SLABS = D_IN // SLAB_K
UNIT_WORDS = 1024

X_ROWS = (0, 1)
SWEEPS = ((2, 3, 4, 5), (6, 7), (8,))

FINE_SLABS = 1
RAW_BUFS = 9
ODD_BUFS = 5
GROUPED_BUFS = 4
CODE_BUFS = 5
BANKS = 8
LAG = 4
FIRST_SWEEP_JOBS = 3
SWAP_AHEAD = 8
SMALL_LOADS_FROM = 53
SMALL_TRANSPOSES_TURN = 26
SMALL_PRODUCTS_TURN = 28

FLOPS = 2 * BATCH * GATES * D_IN + 2 * BATCH * GATES * D_HID


def tile_share_lstm_cell_pa_k_kernel(
    tc, x, h_minors, c_minors, s0, s1, s2, mask, weight_ih, bias_ih, weight_hh, bias_hh,
    weight_sh0, bias_sh0, weight_sh1, bias_sh1, weight_sh2, bias_sh2,
    out_0, out_1, out_2, out_3, out_4,
):
    nc = tc.nc

    units = []
    for s in range(SLABS):
        c = s * SLAB_PASSES
        if s < FINE_SLABS:
            for c in range(c, c + SLAB_PASSES, PAIR):
                units += [(X_ROWS, c, PAIR), (SWEEPS[0], c, PAIR)]
        else:
            units += [(X_ROWS, c, SLAB_PASSES)]
            units += [(SWEEPS[0], c + d, PAIR) for d in range(0, SLAB_PASSES, PAIR)]
    for tiles in SWEEPS[1:]:
        passes = UNIT_WORDS // (P * len(tiles))
        units += [(tiles, c, passes) for c in range(0, N_PASSES, passes)]
    tiles, c, passes = units.pop()
    units += [(tiles, c + d, passes // 2) for d in (0, passes // 2)]
    last_unit = [max(u for u, unit in enumerate(units) if unit[0] == tiles) for tiles in SWEEPS]

    pieces = []
    chunk = 0
    for s in range(SLABS):
        k = s * SLAB_K
        if s < FINE_SLABS:
            for i, k_half in enumerate((k, k + PAIR_K)):
                for j, rt in enumerate(X_ROWS):
                    pieces.append((chunk, (i * X_TILES + j) * PAIR_K, (rt,), k_half, PAIR_K))
                for j, rt in enumerate(SWEEPS[0]):
                    pieces.append((chunk + 1 + i, j * PAIR_K, (rt,), k_half, PAIR_K))
        else:
            for i, tiles in enumerate((X_ROWS, SWEEPS[0][0:2], SWEEPS[0][2:4])):
                pieces += [(chunk + i, j * SLAB_K, (rt,), k, SLAB_K) for j, rt in enumerate(tiles)]
        chunk += 3
    for tiles in SWEEPS[1:]:
        width = CHUNK // len(tiles)
        for k in range(0, D_IN, width):
            pieces.append((chunk, 0, tiles, k, width))
            chunk += 1
    n_chunks = chunk
    piece_of, place_of = {}, {}
    for n, (chunk, first, tiles, k, width) in enumerate(pieces):
        for j, rt in enumerate(tiles):
            for d in range(0, width, PAIR_K):
                piece_of[(rt, (k + d) // PAIR_K)] = n
                place_of[(rt, (k + d) // PAIR_K)] = (chunk, first + j * width + d)
    pieces_needed, chunks_done = [], []
    for tiles, c, passes in units:
        last = max(piece_of[(rt, (c + passes) // PAIR - 1)] for rt in tiles)
        pieces_needed.append(max([last + 1] + pieces_needed))
    oldest = n_chunks
    for tiles, c, passes in reversed(units):
        chunks_done.append(oldest)
        oldest = min([oldest] + [place_of[(rt, c // PAIR)][0] for rt in tiles])
    chunks_done.reverse()

    with ExitStack() as ctx:
        ctx.enter_context(tc.manual_schedule())
        const = ctx.enter_context(tc.tile_pool(name="const", bufs=1))
        raw_pool = ctx.enter_context(tc.tile_pool(name="raw", bufs=RAW_BUFS))
        odd_pool = ctx.enter_context(tc.tile_pool(name="odd", bufs=ODD_BUFS))
        grouped_pool = ctx.enter_context(tc.tile_pool(name="grouped", bufs=GROUPED_BUFS))
        code_pool = ctx.enter_context(tc.tile_pool(name="code", bufs=CODE_BUFS))
        bank_pool = ctx.enter_context(tc.psum_pool(name="bank", bufs=BANKS))

        raw_of = {}

        def load(n):
            chunk, first, tiles, k, width = pieces[n]
            if chunk not in raw_of:
                raw_of[chunk] = raw_pool.tile([P, CHUNK], BF16, name="raw", tag="raw")
            source = x if tiles[0] < X_TILES else weight_ih
            row = (tiles[0] if tiles[0] < X_TILES else tiles[0] - X_TILES) * P
            rows = source[row : row + len(tiles) * P, k : k + width]
            nc.sync.dma_start(
                out=raw_of[chunk][:, first : first + len(tiles) * width].rearrange(
                    "p (t k) -> p t k", t=len(tiles)
                ),
                in_=rows.rearrange("(t p) k -> p t k", p=P),
            )
            if n >= SMALL_LOADS_FROM:
                for tile, source in small_loads[2 * (n - SMALL_LOADS_FROM) :][0:2]:
                    nc.sync.dma_start(out=tile, in_=source)

        def load_more(n, chunks):
            while n < len(pieces) and pieces[n][0] < chunks:
                load(n)
                n += 1
            return n

        n_loaded = load_more(0, RAW_BUFS)

        ident_f32 = const.tile([P, P], F32)
        make_identity(nc, ident_f32[:])
        ident_bf16 = const.tile([P, P], BF16)
        make_identity(nc, ident_bf16[:])
        ones = const.tile([P, P], BF16)
        nc.vector.memset(ones[:], 1.0)
        warm = const.tile([P, 1], F32)
        nc.vector.memset(warm[:], 0.0)
        nc.scalar.activation(out=warm[:], in_=warm[:], func=ACT.Sigmoid)

        x_codes = const.tile([P, N_PASSES * BATCH], U32, align_bytes=64)
        x_scales = const.tile([P, N_PASSES * BATCH], U8, align_bytes=64)

        act_raw = const.tile([P, 4, X_TILES, D_HID], BF16)
        w_raw = const.tile([P, 8, D_HID], BF16)
        nc.vector.memset(w_raw[:, 7, :], 0.0)
        bias_rows = const.tile([P, GATES], BF16)
        nc.vector.memset(bias_rows[:], 0.0)
        c_raw = const.tile([P, X_TILES, D_HID], BF16)

        small_loads = [
            (act_raw[:, j, :, :], act.rearrange("(t p) d -> p t d", p=P))
            for j, act in enumerate((h_minors, s0, s1, s2))
        ]
        small_loads += [(w_raw[:, 0:4, :], weight_hh.rearrange("(j p) d -> p j d", p=P))]
        small_loads += [
            (w_raw[:, 4 + j, :], w_sh) for j, w_sh in enumerate((weight_sh0, weight_sh1, weight_sh2))
        ]
        small_loads += [(c_raw[:], c_minors.rearrange("(t p) d -> p t d", p=P))]

        nc.gpsimd.dma_start(out=w_raw[0:X_TILES, 7, :], in_=mask.rearrange("(t p) -> t p", p=P))
        nc.gpsimd.dma_start(out=bias_rows[0:1, :], in_=bias_ih.rearrange("(o n) -> o n", o=1))
        nc.gpsimd.dma_start(
            out=bias_rows[1:2, 0:LSTM_GATES], in_=bias_hh.rearrange("(o n) -> o n", o=1)
        )
        for j, b_sh in enumerate((bias_sh0, bias_sh1, bias_sh2)):
            cols = slice(LSTM_GATES + j * D_HID, LSTM_GATES + (j + 1) * D_HID)
            nc.gpsimd.dma_start(out=bias_rows[1:2, cols], in_=b_sh.rearrange("(o n) -> o n", o=1))

        odd_of = {}

        def groups_of(n):
            chunk, first, tiles, k, width = pieces[n]
            return raw_of[chunk][:, first : first + len(tiles) * width].rearrange(
                "p (c h g e k) -> p c h g e k", h=HALVES, g=PASS_GROUPS // 4, e=2, k=GROUP_K
            )

        def swap_groups(n):
            chunk, first, tiles, k, width = pieces[n]
            if chunk not in odd_of:
                odd_of[chunk] = odd_pool.tile([P, CHUNK // 2], BF16, name="odd", tag="odd")
            nc.vector.tensor_copy(
                out=odd_of[chunk][:, first // 2 : (first + len(tiles) * width) // 2].rearrange(
                    "p (c g h k) -> p c h g k", g=PASS_GROUPS // 4, h=HALVES, k=GROUP_K
                ),
                in_=groups_of(n)[:, :, :, :, 1, :],
            )

        def swap_back(n):
            groups = groups_of(n)
            nc.vector.tensor_copy(out=groups[:, :, 0, :, 1, :], in_=groups[:, :, 1, :, 0, :])

        grouped_of = {}

        def transpose_unit(u):
            tiles, c, passes = units[u]
            rows = P * len(tiles)
            grouped_of[u] = grouped_pool.tile(
                [P, passes * rows * PACK], BF16, name="grouped", tag="grouped", align_bytes=64
            )
            grouped_words = grouped_of[u][:].bitcast(F32).rearrange(
                "p (a r h) -> p a r h", a=passes, h=HALVES
            )
            for a in range(0, passes, PAIR):
                for j, rt in enumerate(tiles):
                    n, place = place_of[(rt, (c + a) // PAIR)]
                    even_words = raw_of[n][:, place : place + PAIR_K].bitcast(F32)
                    odd_words = odd_of[n][:, place // 2 : (place + PAIR_K) // 2].bitcast(F32)
                    bank = bank_pool.tile([P, PAIR, HALVES, P], F32, name="bank", tag="bank")
                    for b in range(PAIR):
                        nc.tensor.transpose(
                            bank[:, b, 0, :], even_words[:, 2 * b * P : (2 * b + 1) * P], ident_f32[:]
                        )
                        nc.tensor.transpose(
                            bank[:, b, 1, :], odd_words[:, b * P : (b + 1) * P], ident_f32[:]
                        )
                    dst = grouped_words[:, a : a + PAIR, j * P : (j + 1) * P, :]
                    src = bank[:].rearrange("p b h r -> p b r h")
                    if u >= len(units) - 2 and a % (2 * PAIR) == 0:
                        nc.vector.tensor_copy(out=dst, in_=src)
                    else:
                        nc.scalar.copy(out=dst, in_=src)

        codes_of = {}

        def quantise_unit(u):
            tiles, c, passes = units[u]
            n_words = passes * P * len(tiles)
            if tiles == X_ROWS:
                codes = x_codes[:, c * BATCH : c * BATCH + n_words]
                scales = x_scales[:, c * BATCH : c * BATCH + n_words]
            else:
                w_codes = code_pool.tile([P, n_words], U32, name="w_codes", tag="codes", align_bytes=64)
                w_scales = code_pool.tile([P, n_words], U8, name="w_scales", tag="scales", align_bytes=64)
                codes, scales = w_codes[:], w_scales[:]
                codes_of[u] = (w_codes, w_scales)
            nc.vector.quantize_mx(out=codes.bitcast(FP8X4), scales=scales, in_=grouped_of[u][:])

        acc = {}

        def jobs_of_unit(u):
            tiles, c, passes = units[u]
            if tiles == X_ROWS:
                return []
            return [(u, bt, a) for bt in range(X_TILES) for a in range(passes)]

        def multiply(u, bt, a):
            tiles, c, passes = units[u]
            c += a
            w_codes, w_scales = codes_of[u]
            width = P * len(tiles)
            if c == 0:
                acc[(tiles, bt)] = bank_pool.tile([P, width], F32, name="acc", tag="bank")
            x_cols = slice(c * BATCH + bt * P, c * BATCH + (bt + 1) * P)
            w_cols = slice(a * width, (a + 1) * width)
            nc.tensor.matmul_mx(
                out=acc[(tiles, bt)][:],
                lhsT=x_codes[:, x_cols].bitcast(FP8X4),
                lhsT_scale=x_scales[:, x_cols],
                rhs=w_codes[:, w_cols].bitcast(FP8X4),
                rhs_scale=w_scales[:, w_cols],
                start=(c == 0),
                stop=(c == N_PASSES - 1),
            )

        addend = const.tile([P, X_TILES, GATES], F32)
        mask_col = const.tile([P, X_TILES], F32)
        c_masked = const.tile([P, X_TILES, D_HID], F32)
        act_t = const.tile([P, 4 * X_TILES, P], BF16)
        w_t = const.tile([P, 8 * D_HID], BF16)

        def small_transposes():
            act_t_bank = bank_pool.tile([P, 4 * X_TILES, P], BF16, name="act_t_bank", tag="bank")
            for j in range(4):
                for bt in range(X_TILES):
                    nc.tensor.transpose(
                        act_t_bank[:, j * X_TILES + bt, :], act_raw[:, j, bt, :], ident_bf16[:]
                    )
            nc.scalar.copy(out=act_t[:], in_=act_t_bank[:])
            w_t_bank = bank_pool.tile([P, 8 * D_HID], BF16, name="w_t_bank", tag="bank")
            for j in range(8):
                nc.tensor.transpose(
                    w_t_bank[:, j * D_HID : (j + 1) * D_HID], w_raw[:, j, :], ident_bf16[:]
                )
            nc.scalar.copy(out=w_t[:], in_=w_t_bank[:])

        def small_products(bt):
            if bt == 0:
                nc.vector.tensor_copy(out=mask_col[:], in_=w_t[:, GATES : GATES + X_TILES])
            nc.vector.tensor_scalar_mul(
                out=c_masked[:, bt, :], in0=c_raw[:, bt, :], scalar1=mask_col[:, bt : bt + 1]
            )
            lstm = bank_pool.tile([P, LSTM_GATES], F32, name="lstm", tag="bank")
            nc.tensor.matmul(
                out=lstm[:], lhsT=act_t[:, bt, :], rhs=w_t[:, 0:LSTM_GATES], start=True, stop=False
            )
            nc.tensor.matmul(
                out=lstm[:], lhsT=ones[:], rhs=bias_rows[:, 0:LSTM_GATES], start=False, stop=True
            )
            nc.scalar.copy(out=addend[:, bt, 0:LSTM_GATES], in_=lstm[:])
            shared = bank_pool.tile([P, GATES - LSTM_GATES], F32, name="shared", tag="bank")
            for j in range(3):
                cols = slice(LSTM_GATES + j * D_HID, LSTM_GATES + (j + 1) * D_HID)
                group = shared[:, j * D_HID : (j + 1) * D_HID]
                nc.tensor.matmul(
                    out=group, lhsT=act_t[:, (1 + j) * X_TILES + bt, :], rhs=w_t[:, cols],
                    start=True, stop=False,
                )
                nc.tensor.matmul(
                    out=group, lhsT=ones[:], rhs=bias_rows[:, cols], start=False, stop=True
                )
            nc.scalar.copy(out=addend[:, bt, LSTM_GATES:GATES], in_=shared[:])

        def cell_tile(name, blocks=1):
            return const.tile([P, X_TILES, blocks * D_HID], F32, name=name)

        def block(tile, j):
            return tile[:, :, j * D_HID : (j + 1) * D_HID]

        def add_small(sweep, pre):
            tiles = SWEEPS[sweep]
            first = (tiles[0] - X_TILES) * D_HID
            width = len(tiles) * D_HID
            for bt in range(X_TILES):
                nc.vector.tensor_add(
                    out=pre[:, bt, :], in0=acc[(tiles, bt)][:],
                    in1=addend[:, bt, first : first + width],
                )

        def store(queue, out, tile):
            queue.dma_start(out=out.rearrange("(t p) d -> p t d", p=P), in_=tile[:])

        pre_lstm = cell_tile("pre_lstm", 4)
        gate = cell_tile("gate", 4)
        i_g, f_g, o_g, c_hat = [block(gate, j) for j in range(4)]
        kept, fresh, c_t, tanh_c = [cell_tile(n) for n in ("kept", "fresh", "c_t", "tanh_c")]
        tc_m = cell_tile("tc_m")
        h = cell_tile("h")
        less_o = cell_tile("less_o")
        pre_b01 = cell_tile("pre_b01", 2)
        b01 = cell_tile("b01", 2)
        s_0, s_1, s_2 = [cell_tile(n) for n in ("s_0", "s_1", "s_2")]
        rest_1, rest_2 = cell_tile("rest_1"), cell_tile("rest_2")
        pre_b2, b2 = cell_tile("pre_b2"), cell_tile("b2")

        def lstm_sums():
            add_small(0, pre_lstm)

        def lstm_gates():
            nc.scalar.activation(
                out=gate[:, :, 0 : 3 * D_HID], in_=pre_lstm[:, :, 0 : 3 * D_HID], func=ACT.Sigmoid
            )
            nc.scalar.activation(out=c_hat, in_=block(pre_lstm, 3), func=ACT.Tanh)

        def cell_state():
            for bt in range(X_TILES):
                nc.vector.scalar_tensor_tensor(
                    out=fresh[:, bt, :], in0=i_g[:, bt, :], scalar=mask_col[:, bt : bt + 1],
                    in1=c_hat[:, bt, :], op0=ALU.mult, op1=ALU.mult,
                )
            nc.vector.tensor_mul(out=kept[:], in0=f_g, in1=c_masked[:])
            for bt in range(X_TILES):
                nc.vector.tensor_add(out=c_t[:, bt, :], in0=kept[:, bt, :], in1=fresh[:, bt, :])
            store(nc.gpsimd, out_1, c_t)

        def cell_tanh():
            nc.scalar.activation(out=tanh_c[:], in_=c_t[:], func=ACT.Tanh)
            nc.scalar.activation(out=less_o[:], in_=o_g, func=ACT.Identity, scale=-1.0, bias=1.0)
            for bt in range(X_TILES):
                nc.scalar.activation(
                    out=tc_m[:, bt, :], in_=tanh_c[:, bt, :], func=ACT.Copy,
                    scale=mask_col[:, bt : bt + 1],
                )

        def hidden():
            nc.vector.tensor_mul(out=h[:], in0=o_g, in1=tc_m[:])
            store(nc.gpsimd, out_0, h)

        def b01_sums():
            add_small(1, pre_b01)

        def b01_gates():
            nc.scalar.activation(out=b01[:], in_=pre_b01[:], func=ACT.Sigmoid)

        tiles_in_turn = range(X_TILES)

        def shared_01():
            for bt in tiles_in_turn:
                b_j = b01[:, bt, :].rearrange("p (j d) -> p j d", j=2)
                nc.vector.tensor_add(
                    out=b_j, in0=b_j,
                    in1=less_o[:, bt, :].unsqueeze(1).to_broadcast([P, 2, D_HID]),
                )
            for bt in tiles_in_turn:
                nc.vector.tensor_mul(
                    out=s_0[:, bt, :], in0=block(b01, 0)[:, bt, :], in1=tc_m[:, bt, :]
                )
            store(nc.sync, out_2, s_0)
            for bt in tiles_in_turn:
                nc.vector.scalar_tensor_tensor(
                    out=rest_1[:, bt, :], in0=block(b01, 1)[:, bt, :], scalar=1.0,
                    in1=s_0[:, bt, :], op0=ALU.add, op1=ALU.subtract,
                )
            for bt in tiles_in_turn:
                nc.vector.scalar_tensor_tensor(
                    out=s_1[:, bt, :], in0=rest_1[:, bt, :], scalar=0.5, in1=tc_m[:, bt, :],
                    op0=ALU.mult, op1=ALU.mult,
                )
            store(nc.sync, out_3, s_1)
            for bt in tiles_in_turn:
                nc.vector.scalar_tensor_tensor(
                    out=rest_2[:, bt, :], in0=s_0[:, bt, :], scalar=-2.0, in1=less_o[:, bt, :],
                    op0=ALU.mult, op1=ALU.add,
                )
            for bt in tiles_in_turn:
                nc.vector.scalar_tensor_tensor(
                    out=rest_2[:, bt, :], in0=rest_2[:, bt, :], scalar=2.0, in1=s_1[:, bt, :],
                    op0=ALU.add, op1=ALU.subtract,
                )

        def shared_2():
            add_small(2, pre_b2)
            for bt in tiles_in_turn:
                nc.scalar.activation(out=b2[:, bt, :], in_=pre_b2[:, bt, :], func=ACT.Sigmoid)
            for bt in tiles_in_turn:
                nc.vector.tensor_add(
                    out=rest_2[:, bt, :], in0=b2[:, bt, :], in1=rest_2[:, bt, :]
                )
            for bt in tiles_in_turn:
                nc.vector.scalar_tensor_tensor(
                    out=s_2[:, bt, :], in0=rest_2[:, bt, :], scalar=1.0 / 3.0, in1=tc_m[:, bt, :],
                    op0=ALU.mult, op1=ALU.mult,
                )
                nc.sync.dma_start(out=out_4[bt * P : (bt + 1) * P, :], in_=s_2[:, bt, :])

        steps = {SMALL_TRANSPOSES_TURN: [small_transposes]}
        for bt in range(X_TILES):
            steps[SMALL_PRODUCTS_TURN + bt] = [lambda bt=bt: small_products(bt)]
        for sweep, chain in enumerate((
            (lstm_sums, lstm_gates, cell_state, cell_tanh, hidden),
            (b01_sums, b01_gates, shared_01),
            (shared_2,),
        )):
            first_turn = last_unit[sweep] + LAG
            if sweep == 0:
                first_turn = max(first_turn, SMALL_PRODUCTS_TURN + X_TILES)
            for d, step in enumerate(chain):
                steps.setdefault(first_turn + d, []).append(step)

        jobs = []
        n_swapped = 0
        halves_swapped = 0
        halves_used = 0
        for turn in range(len(units) + LAG):
            half_swapped = []
            if turn < len(units):
                tiles, c, passes = units[turn]
                halves_used += len(tiles) * passes // PAIR
                while n_swapped < len(pieces) and (
                    n_swapped < pieces_needed[turn] or halves_swapped < halves_used + SWAP_AHEAD
                ):
                    swap_groups(n_swapped)
                    for n in half_swapped:
                        swap_back(n)
                    half_swapped = []
                    if n_swapped < pieces_needed[turn]:
                        swap_back(n_swapped)
                    else:
                        half_swapped.append(n_swapped)
                    chunk, first, tiles, k, width = pieces[n_swapped]
                    halves_swapped += len(tiles) * width // PAIR_K
                    n_swapped += 1
                transpose_unit(turn)
                n_loaded = load_more(n_loaded, chunks_done[turn] + RAW_BUFS)
            if 0 < turn <= len(units):
                quantise_unit(turn - 1)
            for n in half_swapped:
                swap_back(n)
            if turn >= LAG:
                jobs += jobs_of_unit(turn - LAG)
            n_jobs = FIRST_SWEEP_JOBS if turn - LAG < last_unit[0] else len(jobs)
            for job in jobs[:n_jobs]:
                multiply(*job)
            jobs = jobs[n_jobs:]
            for step in steps.get(turn, []):
                step()
